import numpy as np
import ml_dtypes


def mxq(x, axis, fmt="e4m3"):
    dtype, down = {"e4m3": (ml_dtypes.float8_e4m3fn, 7), "e5m2": (ml_dtypes.float8_e5m2, 14)}[fmt]
    v = np.moveaxis(np.asarray(x, np.float32).astype(ml_dtypes.bfloat16).astype(np.float64), axis, -1)
    blocks = v.reshape(v.shape[:-1] + (-1, 32))
    amax = np.abs(blocks).max(-1, keepdims=True)
    byte = np.maximum(np.where(amax > 0, np.frexp(amax)[1] - 1 + 127, 0) - down, 1)
    scale = np.exp2(byte - 127.0)
    codes = (blocks / scale).astype(np.float32).astype(dtype).astype(np.float64)
    return np.moveaxis((codes * scale).reshape(v.shape), -1, axis)


WIDE = False


def mx_kscale(k):
    if not WIDE:
        return np.ones(k)
    levels = np.array([10, -10, 5, -5, 0])
    a = np.random.permutation(np.resize(levels, k // 512 * 4)).reshape(k // 512, 4)
    idx = np.arange(k)
    return np.exp2(a[idx // 512, idx % 128 // 32])


BF16 = ml_dtypes.bfloat16


def bf(x):
    return np.asarray(x, np.float32).astype(BF16)


def f64(x):
    return np.asarray(x).astype(np.float64)


B, P, DIN, COND, HID, HA, HB, HC, OUT = 4, 256, 3, 48, 1024, 1024, 1024, 1024, 257
N = B * P
INV_SQRT2 = np.sqrt(0.5)


def softplus_beta100(v):
    z = 100.0 * v
    return (np.maximum(z, 0.0) + np.log(1.0 + np.exp(-np.abs(z)))) * 0.01


def setup_inputs():
    s = mx_kscale(HA)
    return {"h3": bf(softplus_beta100(0.03 + 0.016 * np.random.standard_normal((N, HA - DIN))) * s[:HA - DIN]),
            "x_in": bf(np.random.uniform(-1.0, 1.0, (N, DIN)) * s[HA - DIN:]),
            "W4": bf(np.random.standard_normal((HB, HA)) * 0.42 / np.sqrt(HA) / s[None, :]),
            "b4": bf(0.03 + 0.005 * np.random.standard_normal(HB)),
            "W5": bf(np.random.standard_normal((HC, HB)) * 2.6 / np.sqrt(HB)),
            "b5": bf(np.random.standard_normal(HC) * 0.04)}


def reference(h3, x_in, W4, b4, W5, b5):
    x = np.concatenate([f64(h3), f64(x_in)], axis=-1) * INV_SQRT2
    h4 = softplus_beta100((mxq(x, 1, "e4m3") @ mxq(f64(W4), 1, "e4m3").T) + f64(b4))
    return softplus_beta100((mxq(h4, 1, "e4m3") @ mxq(f64(W5), 1, "e4m3").T) + f64(b5))

@@ -1,0 +1,317 @@
+import math
+from contextlib import ExitStack
+
+import concourse.mybir as mybir
+from concourse.masks import make_identity
+
+F32 = mybir.dt.float32
+BF16 = mybir.dt.bfloat16
+U32 = mybir.dt.uint32
+U8 = mybir.dt.uint8
+FP8X4 = mybir.dt.float8_e4m3fn_x4
+ACT = mybir.ActivationFunctionType
+ALU = mybir.AluOpType
+
+P = 128
+N_TOK = 1024
+K = 1024
+H3_COLS = 1021
+DMA_COLS = 1008
+NT = 8
+FLOPS = 2 * 2 * 1024 * 1024 * 1024
+
+V_EVACS = (("w5", 1), ("w5", 3), ("w5", 5))
+
+
+def tile_implicitnet_pa_kernel(tc, h3, x_in, W4, b4, W5, b5, out):
+    nc = tc.nc
+    with ExitStack() as ctx:
+        const = ctx.enter_context(tc.tile_pool(name="const", bufs=1))
+        raw = ctx.enter_context(tc.tile_pool(name="raw", bufs=1))
+        codes = ctx.enter_context(tc.tile_pool(name="codes", bufs=1))
+        grp_pool = ctx.enter_context(tc.tile_pool(name="grp", bufs=6))
+        xsc_pool = ctx.enter_context(tc.tile_pool(name="xsc", bufs=3))
+        h4g_pool = ctx.enter_context(tc.tile_pool(name="h4g", bufs=3))
+        act = ctx.enter_context(tc.tile_pool(name="act", bufs=1))
+        ps_tr = ctx.enter_context(tc.psum_pool(name="ps_tr", bufs=3))
+        ps_mm = ctx.enter_context(tc.psum_pool(name="ps_mm", bufs=5))
+
+        ident = const.tile([P, P], F32, name="ident")
+        make_identity(nc, ident[:])
+
+        ctx.enter_context(tc.manual_schedule())
+
+        x_raw = raw.tile([P, NT, K], BF16, name="x_raw")
+        tail = raw.tile([P, NT, 16], BF16, name="tail")
+        xin = raw.tile([P, NT, 4], BF16, name="xin")
+        w4_raw = raw.tile([P, 4, 2, K], BF16, name="w4_raw")
+        w5_raw = raw.tile([P, NT, K], BF16, name="w5_raw")
+        b4r = const.tile([P, 4, 2], BF16, name="b4r")
+        b4g = const.tile([P, 8], F32, name="b4g")
+        b5bc = const.tile([P, K], BF16, name="b5bc")
+        delta = const.tile([P, 1], F32, name="delta")
+        warm = const.tile([P, 1], F32, name="warm")
+
+        xc = codes.tile([P, NT * 256], U32, name="xc", align_bytes=64)
+        xs = codes.tile([P, NT * 256], U8, name="xs", align_bytes=64)
+        w4c = codes.tile([P, NT * 256], U32, name="w4c", align_bytes=64)
+        w4s = codes.tile([P, NT * 256], U8, name="w4s", align_bytes=64)
+        w5c = codes.tile([P, 2048], U32, name="w5c", align_bytes=64)
+        w5s = codes.tile([P, 2048], U8, name="w5s", align_bytes=64)
+        h4c = codes.tile([P, NT * 256], U32, name="h4c", align_bytes=64)
+        h4s = codes.tile([P, NT * 256], U8, name="h4s", align_bytes=64)
+        w5g = [
+            raw.tile([P, 4096], BF16, name="w5g%d" % h, align_bytes=64) for h in range(2)
+        ]
+        v = [act.tile([P, K], F32, name="v%d" % t) for t in range(NT)]
+        s = [act.tile([P, K], F32, name="s%d" % t) for t in range(NT)]
+
+        nc.scalar.dma_start(
+            out=tail[:, :, 0:13],
+            in_=h3[:, DMA_COLS:H3_COLS].rearrange("(t p) c -> p t c", p=P),
+        )
+        nc.scalar.dma_start(out=xin[:, :, 0:3], in_=x_in.rearrange("(t p) c -> p t c", p=P))
+        nc.scalar.dma_start(out=b4r[:], in_=b4.rearrange("(a p e) -> p a e", a=4, p=P, e=2))
+
+        def load_w4(a):
+            nc.sync.dma_start(
+                out=w4_raw[:, a, :, :],
+                in_=W4[a * 256 : (a + 1) * 256, :].rearrange("(p e) k -> p e k", e=2),
+            )
+
+        def load_x(t):
+            nc.sync.dma_start(
+                out=x_raw[:, t, 0:DMA_COLS], in_=h3[t * P : (t + 1) * P, 0:DMA_COLS]
+            )
+
+        load_w4(0)
+        load_w4(1)
+        for t in range(4):
+            load_x(t)
+        load_w4(2)
+        load_w4(3)
+        for t in range(4, 8):
+            load_x(t)
+        for c in range(4):
+            nc.sync.dma_start(
+                out=w5_raw[:, 2 * c : 2 * c + 2, :],
+                in_=W5[c * 256 : (c + 1) * 256, :].rearrange("(t p) k -> p t k", p=P),
+            )
+        nc.sync.dma_start(out=b5bc[:], in_=b5.partition_broadcast(P))
+
+        nc.vector.memset(warm[:], 0.0)
+        nc.vector.memset(delta[:], 2.0 ** -60)
+        nc.scalar.activation(out=warm[:], in_=warm[:], func=ACT.Sigmoid)
+        nc.vector.tensor_copy(out=x_raw[:, :, DMA_COLS:H3_COLS], in_=tail[:, :, 0:13])
+        nc.vector.tensor_copy(out=x_raw[:, :, H3_COLS:K], in_=xin[:, :, 0:3])
+        nc.vector.tensor_copy(out=b4g[:], in_=b4r[:].rearrange("p a e -> p (a e)"))
+
+        banks = {}
+        grps = {}
+
+        def row_src(row):
+            kind, i = row
+            if kind == "x":
+                return x_raw[:, i, :]
+            if kind == "w4":
+                return w4_raw[:, i // 2, i % 2, :]
+            return w5_raw[:, i, :]
+
+        def do_t(row):
+            words = row_src(row).bitcast(F32)
+            bank = ps_tr.tile([P, 512], F32, name="tr", tag="tr")
+            for c in range(4):
+                nc.tensor.transpose(
+                    bank[:, c * P : (c + 1) * P], words[:, c * P : (c + 1) * P], ident[:]
+                )
+            banks[row] = bank
+
+        def do_e(row):
+            kind, i = row
+            src = banks[row][:].rearrange("p (k u r) -> p k r u", k=2, u=2)
+            if kind == "w5":
+                dst = (
+                    w5g[i // 4][:]
+                    .bitcast(F32)
+                    .rearrange("p (g c u) -> p g c u", g=2, u=2)[
+                        :, :, (i % 4) * P : (i % 4 + 1) * P, :
+                    ]
+                )
+            else:
+                g_t = grp_pool.tile([P, K], BF16, name="grp", tag="grp", align_bytes=64)
+                grps[row] = g_t
+                dst = g_t[:].bitcast(F32).rearrange("p (k r u) -> p k r u", k=2, u=2)
+            if row in V_EVACS:
+                nc.vector.tensor_copy(out=dst, in_=src)
+            else:
+                nc.scalar.copy(out=dst, in_=src)
+
+        def do_m(row):
+            x_t = xsc_pool.tile([P, K], BF16, name="xsc", tag="xsc", align_bytes=64)
+            nc.vector.tensor_scalar(
+                out=x_t[:], in0=grps[row][:], scalar1=math.sqrt(0.5), scalar2=None, op0=ALU.mult
+            )
+            grps[row] = x_t
+
+        def do_q(row):
+            kind, i = row
+            if kind == "w5":
+                h = i // 4
+                nc.vector.quantize_mx(
+                    out=w5c[:, h * 1024 : (h + 1) * 1024].bitcast(FP8X4),
+                    scales=w5s[:, h * 1024 : (h + 1) * 1024],
+                    in_=w5g[h][:],
+                )
+                return
+            cd, sc = (xc, xs) if kind == "x" else (w4c, w4s)
+            nc.vector.quantize_mx(
+                out=cd[:, i * 256 : (i + 1) * 256].bitcast(FP8X4),
+                scales=sc[:, i * 256 : (i + 1) * 256],
+                in_=grps[row][:],
+            )
+
+        def do_mm1(unit):
+            g, t = unit
+            bank = ps_mm.tile([P, 512], F32, name="mm", tag="mm")
+            for j in range(4):
+                for kg in range(2):
+                    wo = ((g * 4 + j) * 2 + kg) * P
+                    xo = (t * 2 + kg) * P
+                    nc.tensor.matmul_mx(
+                        out=bank[:, j * P : (j + 1) * P],
+                        lhsT=w4c[:, wo : wo + P].bitcast(FP8X4),
+                        lhsT_scale=w4s[:, wo : wo + P],
+                        rhs=xc[:, xo : xo + P].bitcast(FP8X4),
+                        rhs_scale=xs[:, xo : xo + P],
+                        start=(kg == 0),
+                        stop=(kg == 1),
+                    )
+            banks[unit] = bank
+
+        def do_v1(unit):
+            g, t = unit
+            nc.vector.tensor_tensor(
+                out=v[t][:, g * 512 : (g + 1) * 512].rearrange("p (w j) -> p w j", j=4),
+                in0=banks[unit][:].rearrange("p (j w) -> p w j", j=4),
+                in1=b4g[:, g * 4 : (g + 1) * 4].unsqueeze(1).to_broadcast([P, P, 4]),
+                op=ALU.add,
+            )
+
+        def do_s1(unit):
+            g, t = unit
+            nc.scalar.activation(
+                out=s[t][:, g * 512 : (g + 1) * 512],
+                in_=v[t][:, g * 512 : (g + 1) * 512],
+                func=ACT.Sigmoid,
+                scale=-100.0,
+            )
+
+        rows = (
+            [("w4", i) for i in range(4)]
+            + [("x", t) for t in range(4)]
+            + [("w4", i) for i in range(4, 8)]
+            + [("x", t) for t in range(4, 8)]
+            + [("w5", r) for r in range(8)]
+        )
+        plan = {}
+
+        def at(step, stage, item):
+            plan[(step, stage)] = plan.get((step, stage), []) + [item]
+
+        q_step = {}
+        for i, row in enumerate(rows):
+            at(i, "t", row)
+            at(i + 1, "e", row)
+            if row[0] == "x":
+                at(i + 2, "m", row)
+                at(i + 3, "q", row)
+                q_step[row] = i + 3
+            elif row[0] == "w4":
+                at(i + 2, "q", row)
+                q_step[row] = i + 2
+            elif row[1] % 4 == 3:
+                at(i + 2, "q", row)
+        last = 0
+        unit_list = (
+            [(0, t) for t in range(4)]
+            + [(1, t) for t in range(4)]
+            + [(g, t) for t in range(4, 8) for g in range(2)]
+        )
+        for unit in unit_list:
+            g, t = unit
+            ready = max(q_step[("x", t)], q_step[("w4", g * 4 + 3)]) + 1
+            at(ready, "mm1", unit)
+            at(ready + 1, "v1", unit)
+            at(ready + 2, "s1", unit)
+            last = max(last, ready + 2)
+        last = max(last, len(rows) + 2)
+        stages = (
+            ("s1", do_s1),
+            ("v1", do_v1),
+            ("mm1", do_mm1),
+            ("q", do_q),
+            ("m", do_m),
+            ("e", do_e),
+            ("t", do_t),
+        )
+        for step in range(last + 1):
+            for stage, fn in stages:
+                for item in plan.get((step, stage), []):
+                    fn(item)
+
+        def softplus_end(dst, t):
+            nc.vector.scalar_tensor_tensor(
+                out=dst, in0=s[t][:], scalar=-0.01, in1=v[t][:], op0=ALU.mult, op1=ALU.max
+            )
+
+        def do_ln(t):
+            nc.scalar.activation(out=s[t][:], in_=s[t][:], func=ACT.Ln, bias=delta[:, 0:1])
+
+        def do_mm2(t, hh):
+            bank = ps_mm.tile([P, 512], F32, name="mm", tag="mm")
+            for g in range(2):
+                ho = (t * 2 + g) * P
+                wo = (hh * 2 + g) * 512
+                nc.tensor.matmul_mx(
+                    out=bank[:],
+                    lhsT=h4c[:, ho : ho + P].bitcast(FP8X4),
+                    lhsT_scale=h4s[:, ho : ho + P],
+                    rhs=w5c[:, wo : wo + 512].bitcast(FP8X4),
+                    rhs_scale=w5s[:, wo : wo + 512],
+                    start=(g == 0),
+                    stop=(g == 1),
+                )
+            banks[("l2", t, hh)] = bank
+
+        def do_v2(t, hh):
+            nc.vector.tensor_tensor(
+                out=v[t][:, hh * 512 : (hh + 1) * 512],
+                in0=banks[("l2", t, hh)][:],
+                in1=b5bc[:, hh * 512 : (hh + 1) * 512],
+                op=ALU.add,
+            )
+
+        for t in range(NT + 2):
+            if t < NT:
+                do_ln(t)
+                h_t = h4g_pool.tile([P, K], BF16, name="h4g", tag="h4g", align_bytes=64)
+                softplus_end(h_t[:], t)
+            if t >= 2:
+                do_v2(t - 2, 0)
+                do_v2(t - 2, 1)
+            if t < NT:
+                nc.vector.quantize_mx(
+                    out=h4c[:, t * 256 : (t + 1) * 256].bitcast(FP8X4),
+                    scales=h4s[:, t * 256 : (t + 1) * 256],
+                    in_=h_t[:],
+                )
+                do_mm2(t, 0)
+                do_mm2(t, 1)
+
+        for t in range(NT):
+            nc.scalar.activation(out=s[t][:], in_=v[t][:], func=ACT.Sigmoid, scale=-100.0)
+
+        for t in range(NT):
+            do_ln(t)
+            softplus_end(s[t][:], t)
+            nc.sync.dma_start(out=out[t * P : (t + 1) * P, :], in_=s[t][:])

@@ -13,14 +13,75 @@ ACT = mybir.ActivationFunctionType
 ALU = mybir.AluOpType
 
 P = 128
-N_TOK = 1024
 K = 1024
 H3_COLS = 1021
 DMA_COLS = 1008
 NT = 8
 FLOPS = 2 * 2 * 1024 * 1024 * 1024
+N_TR = 4
+N_MM = 4
+N_GRP = 10
+N_XSC = 4
+N_H4G = 4
 
-V_EVACS = (("w5", 1), ("w5", 3), ("w5", 5))
+LOADS = ("w4t0", "w4t1", "w4t2", "w4t3", "small", "x0", "x1", "x2", "x3", "x4", "x5", "x6", "x7", "w4t4", "w4t5", "w4t6", "w4t7", "w5c0", "w5c1", "w5c2", "w5c3", "b5")
+PE_ORDER = (
+    ("t", ("w4", 0)), ("t", ("w4", 1)), ("t", ("w4", 2)), ("t", ("w4", 3)),
+    ("t", ("x", 0)), ("t", ("x", 1)), ("t", ("x", 2)), ("t", ("x", 3)),
+    ("mm1", (0, 0)), ("t", ("x", 4)), ("t", ("x", 5)), ("mm1", (0, 1)),
+    ("t", ("x", 6)), ("mm1", (0, 2)), ("t", ("x", 7)), ("mm1", (0, 3)),
+    ("t", ("w4", 4)), ("mm1", (0, 4)), ("t", ("w4", 5)), ("mm1", (0, 5)),
+    ("t", ("w4", 6)), ("mm1", (0, 6)), ("t", ("w4", 7)), ("mm1", (0, 7)),
+    ("t", ("w5", 0)), ("t", ("w5", 1)), ("t", ("w5", 2)), ("t", ("w5", 3)),
+    ("mm1", (1, 0)), ("mm1", (1, 1)), ("mm1", (1, 2)), ("mm1", (1, 3)),
+    ("mm1", (1, 4)), ("mm1", (1, 5)), ("mm1", (1, 6)), ("mm1", (1, 7)),
+    ("t", ("w5", 4)), ("t", ("w5", 5)), ("t", ("w5", 6)), ("t", ("w5", 7)),
+    ("mm2", (0, 0)), ("mm2", (1, 0)), ("mm2", (2, 0)), ("mm2", (3, 0)),
+    ("mm2", (5, 0)), ("mm2", (4, 0)), ("mm2", (6, 0)), ("mm2", (7, 0)),
+    ("mm2", (0, 1)), ("mm2", (1, 1)), ("mm2", (2, 1)), ("mm2", (3, 1)),
+    ("mm2", (4, 1)), ("mm2", (5, 1)), ("mm2", (6, 1)), ("mm2", (7, 1)),
+)
+ACT_ORDER = (
+    ("e", ("w4", 0)), ("e", ("w4", 1)), ("e", ("w4", 2)), ("e", ("w4", 3)),
+    ("e", ("x", 1)), ("e", ("x", 2)), ("e", ("x", 3)), ("e", ("x", 4)),
+    ("e", ("x", 5)), ("e", ("x", 6)), ("e", ("x", 7)), ("e", ("w4", 4)),
+    ("e", ("w4", 5)), ("e", ("w4", 6)), ("s1", ((0, 0), (0, 1),)), ("e", ("w4", 7)),
+    ("s1", ((0, 2), (0, 3),)), ("s1", ((0, 4), (0, 5),)), ("s1", ((0, 6), (0, 7),)), ("s1", ((1, 0), (1, 1),)),
+    ("s1", ((1, 2), (1, 3),)), ("s1", ((1, 4), (1, 5),)), ("s1", ((1, 6), (1, 7),)), ("ln1", ((0, 0), (0, 1),)),
+    ("ln1", ((1, 0), (1, 1),)), ("ln1", ((0, 2), (0, 3),)), ("ln1", ((1, 2), (1, 3),)), ("ln1", ((0, 4), (0, 5),)),
+    ("ln1", ((1, 4), (1, 5),)), ("ln1", ((0, 6), (0, 7),)), ("ln1", ((1, 6), (1, 7),)), ("e", ("w5", 4)),
+    ("e", ("w5", 5)), ("e", ("w5", 6)), ("e", ("w5", 7)), ("s2", ((0, 0), (1, 0),)),
+    ("s2", ((2, 0), (3, 0),)), ("s2", ((4, 0), (5, 0),)), ("s2", ((6, 0), (7, 0),)), ("s2", ((0, 1), (1, 1),)),
+    ("s2", ((2, 1), (3, 1),)), ("s2", ((4, 1), (5, 1),)), ("s2", ((6, 1), (7, 1),)), ("ln2", ((0, 0),)),
+    ("ln2", ((0, 1),)), ("ln2", ((1, 0), (1, 1),)), ("ln2", ((2, 0), (2, 1),)), ("ln2", ((3, 0), (3, 1),)),
+    ("ln2", ((4, 0), (4, 1),)), ("ln2", ((5, 0), (5, 1),)), ("ln2", ((6, 0), (6, 1),)), ("ln2", ((7, 0),)),
+    ("ln2", ((7, 1),)),
+)
+DVE_ORDER = (
+    ("q", (("w4", 0),)), ("q", (("w4", 1),)), ("fix", 0), ("q", (("w4", 2),)),
+    ("q", (("w4", 3),)), ("e", ("x", 0)), ("m", 0), ("q", (("x", 0),)),
+    ("m", 1), ("q", (("x", 1),)), ("m", 2), ("q", (("x", 2),)),
+    ("m", 3), ("v1", (0, 0)), ("m", 4), ("q", (("x", 3),)),
+    ("v1", (0, 1)), ("m", 5), ("q", (("x", 4),)), ("v1", (0, 2)),
+    ("m", 6), ("q", (("x", 5),)), ("v1", (0, 3)), ("m", 7),
+    ("q", (("x", 6),)), ("v1", (0, 4)), ("q", (("x", 7),)), ("q", (("w4", 4),)),
+    ("q", (("w4", 5),)), ("q", (("w4", 6),)), ("v1", (0, 7)), ("q", (("w4", 7),)),
+    ("v1", (0, 5)), ("v1", (0, 6)), ("v1", (1, 0)), ("v1", (1, 1)),
+    ("v1", (1, 2)), ("v1", (1, 3)), ("v1", (1, 4)), ("v1", (1, 5)),
+    ("v1", (1, 6)), ("v1", (1, 7)), ("e", ("w5", 0)), ("e", ("w5", 1)),
+    ("e", ("w5", 2)), ("e", ("w5", 3)), ("q", (("w5", 0), ("w5", 1), ("w5", 2), ("w5", 3),)), ("f1", ((0, 0), (0, 1),)),
+    ("f1", ((1, 0), (1, 1),)), ("q1", ((0, 0), (0, 1),)), ("q1", ((1, 0), (1, 1),)), ("f1", ((0, 2), (0, 3),)),
+    ("f1", ((1, 2), (1, 3),)), ("v2", (0, 0)), ("v2", (1, 0)), ("q1", ((0, 2), (0, 3),)),
+    ("q1", ((1, 2), (1, 3),)), ("f1", ((0, 4), (0, 5),)), ("f1", ((1, 4), (1, 5),)), ("v2", (2, 0)),
+    ("v2", (3, 0)), ("q1", ((0, 4), (0, 5),)), ("q1", ((1, 4), (1, 5),)), ("f1", ((0, 6), (0, 7),)),
+    ("f1", ((1, 6), (1, 7),)), ("v2", (5, 0)), ("q1", ((0, 6), (0, 7),)), ("q1", ((1, 6), (1, 7),)),
+    ("q", (("w5", 4), ("w5", 5), ("w5", 6), ("w5", 7),)), ("v2", (4, 0)), ("v2", (7, 0)), ("v2", (6, 0)),
+    ("v2", (0, 1)), ("v2", (1, 1)), ("v2", (2, 1)), ("v2", (3, 1)),
+    ("v2", (4, 1)), ("v2", (5, 1)), ("v2", (6, 1)), ("v2", (7, 1)),
+    ("f2", ((0, 0),)), ("f2", ((0, 1),)), ("f2", ((1, 0), (1, 1),)), ("f2", ((2, 0), (2, 1),)),
+    ("f2", ((3, 0), (3, 1),)), ("f2", ((4, 0), (4, 1),)), ("f2", ((5, 0), (5, 1),)), ("f2", ((6, 0), (6, 1),)),
+    ("f2", ((7, 0),)), ("f2", ((7, 1),)),
+)
 
 
 def tile_implicitnet_pa_kernel(tc, h3, x_in, W4, b4, W5, b5, out):
@@ -29,12 +90,12 @@ def tile_implicitnet_pa_kernel(tc, h3, x_in, W4, b4, W5, b5, out):
         const = ctx.enter_context(tc.tile_pool(name="const", bufs=1))
         raw = ctx.enter_context(tc.tile_pool(name="raw", bufs=1))
         codes = ctx.enter_context(tc.tile_pool(name="codes", bufs=1))
-        grp_pool = ctx.enter_context(tc.tile_pool(name="grp", bufs=6))
-        xsc_pool = ctx.enter_context(tc.tile_pool(name="xsc", bufs=3))
-        h4g_pool = ctx.enter_context(tc.tile_pool(name="h4g", bufs=3))
+        grp_pool = ctx.enter_context(tc.tile_pool(name="grp", bufs=N_GRP))
+        xsc_pool = ctx.enter_context(tc.tile_pool(name="xsc", bufs=N_XSC))
+        h4g_pool = ctx.enter_context(tc.tile_pool(name="h4g", bufs=N_H4G))
         act = ctx.enter_context(tc.tile_pool(name="act", bufs=1))
-        ps_tr = ctx.enter_context(tc.psum_pool(name="ps_tr", bufs=3))
-        ps_mm = ctx.enter_context(tc.psum_pool(name="ps_mm", bufs=5))
+        ps_tr = ctx.enter_context(tc.psum_pool(name="ps_tr", bufs=N_TR))
+        ps_mm = ctx.enter_context(tc.psum_pool(name="ps_mm", bufs=N_MM))
 
         ident = const.tile([P, P], F32, name="ident")
         make_identity(nc, ident[:])
@@ -58,56 +119,77 @@ def tile_implicitnet_pa_kernel(tc, h3, x_in, W4, b4, W5, b5, out):
         w4s = codes.tile([P, NT * 256], U8, name="w4s", align_bytes=64)
         w5c = codes.tile([P, 2048], U32, name="w5c", align_bytes=64)
         w5s = codes.tile([P, 2048], U8, name="w5s", align_bytes=64)
-        h4c = codes.tile([P, NT * 256], U32, name="h4c", align_bytes=64)
-        h4s = codes.tile([P, NT * 256], U8, name="h4s", align_bytes=64)
+        h4c = codes.tile([P, 16 * P], U32, name="h4c", align_bytes=64)
+        h4s = codes.tile([P, 16 * P], U8, name="h4s", align_bytes=64)
         w5g = [
             raw.tile([P, 4096], BF16, name="w5g%d" % h, align_bytes=64) for h in range(2)
         ]
-        v = [act.tile([P, K], F32, name="v%d" % t) for t in range(NT)]
-        s = [act.tile([P, K], F32, name="s%d" % t) for t in range(NT)]
+        v_all = act.tile([P, 2, NT, 512], F32, name="v_all")
+        s_all = act.tile([P, 2, NT, 512], F32, name="s_all")
 
-        nc.scalar.dma_start(
-            out=tail[:, :, 0:13],
-            in_=h3[:, DMA_COLS:H3_COLS].rearrange("(t p) c -> p t c", p=P),
-        )
-        nc.scalar.dma_start(out=xin[:, :, 0:3], in_=x_in.rearrange("(t p) c -> p t c", p=P))
-        nc.scalar.dma_start(out=b4r[:], in_=b4.rearrange("(a p e) -> p a e", a=4, p=P, e=2))
-
-        def load_w4(a):
-            nc.sync.dma_start(
-                out=w4_raw[:, a, :, :],
-                in_=W4[a * 256 : (a + 1) * 256, :].rearrange("(p e) k -> p e k", e=2),
-            )
-
-        def load_x(t):
-            nc.sync.dma_start(
-                out=x_raw[:, t, 0:DMA_COLS], in_=h3[t * P : (t + 1) * P, 0:DMA_COLS]
-            )
-
-        load_w4(0)
-        load_w4(1)
-        for t in range(4):
-            load_x(t)
-        load_w4(2)
-        load_w4(3)
-        for t in range(4, 8):
-            load_x(t)
-        for c in range(4):
-            nc.sync.dma_start(
-                out=w5_raw[:, 2 * c : 2 * c + 2, :],
-                in_=W5[c * 256 : (c + 1) * 256, :].rearrange("(t p) k -> p t k", p=P),
-            )
-        nc.sync.dma_start(out=b5bc[:], in_=b5.partition_broadcast(P))
+        for name in LOADS:
+            if name == "small":
+                nc.sync.dma_start(
+                    out=tail[:, :, 0:13],
+                    in_=h3[:, DMA_COLS:H3_COLS].rearrange("(t p) c -> p t c", p=P),
+                )
+                nc.sync.dma_start(
+                    out=xin[:, :, 0:3], in_=x_in.rearrange("(t p) c -> p t c", p=P)
+                )
+                nc.sync.dma_start(
+                    out=b4r[:], in_=b4.rearrange("(a p e) -> p a e", a=4, p=P, e=2)
+                )
+            elif name == "b5":
+                nc.sync.dma_start(out=b5bc[:], in_=b5.partition_broadcast(P))
+            elif name[0:3] == "w4t":
+                i = int(name[3:])
+                nc.sync.dma_start(
+                    out=w4_raw[:, i // 2, i % 2, :],
+                    in_=W4[(i // 2) * 256 : (i // 2 + 1) * 256, :].rearrange(
+                        "(p e) k -> p e k", e=2
+                    )[:, i % 2, :],
+                )
+            elif name[0:3] == "w5c":
+                c = int(name[3:])
+                nc.sync.dma_start(
+                    out=w5_raw[:, 2 * c : 2 * c + 2, :],
+                    in_=W5[c * 256 : (c + 1) * 256, :].rearrange("(t p) k -> p t k", p=P),
+                )
+            else:
+                t = int(name[1:])
+                nc.sync.dma_start(
+                    out=x_raw[:, t, 0:DMA_COLS], in_=h3[t * P : (t + 1) * P, 0:DMA_COLS]
+                )
 
         nc.vector.memset(warm[:], 0.0)
         nc.vector.memset(delta[:], 2.0 ** -60)
         nc.scalar.activation(out=warm[:], in_=warm[:], func=ACT.Sigmoid)
-        nc.vector.tensor_copy(out=x_raw[:, :, DMA_COLS:H3_COLS], in_=tail[:, :, 0:13])
-        nc.vector.tensor_copy(out=x_raw[:, :, H3_COLS:K], in_=xin[:, :, 0:3])
-        nc.vector.tensor_copy(out=b4g[:], in_=b4r[:].rearrange("p a e -> p (a e)"))
 
+        done = set()
         banks = {}
         grps = {}
+        tr_hist = []
+        mm_hist = []
+        grp_hist = []
+        xsc_hist = []
+        h4g_hist = []
+
+        def have(keys):
+            return all(k in done for k in keys)
+
+        def slot_free(hist, depth):
+            return len(hist) < depth or ("rel", hist[len(hist) - depth]) in done
+
+        def view(big, units):
+            if len(units) == 1:
+                return big[:, units[0][0], units[0][1], :]
+            if units[0][0] == units[1][0]:
+                a = units[0][0]
+                return big[:, a, units[0][1] : units[-1][1] + 1, :].rearrange("p t c -> p (t c)")
+            return big[:, :, units[0][1], :]
+
+        def l2u(units):
+            return tuple((hh, t) for (t, hh) in units)
 
         def row_src(row):
             kind, i = row
@@ -117,7 +199,16 @@ def tile_implicitnet_pa_kernel(tc, h3, x_in, W4, b4, W5, b5, out):
                 return w4_raw[:, i // 2, i % 2, :]
             return w5_raw[:, i, :]
 
-        def do_t(row):
+        def op_fix(arg, eng):
+            nc.vector.tensor_copy(out=x_raw[:, :, DMA_COLS:H3_COLS], in_=tail[:, :, 0:13])
+            nc.vector.tensor_copy(out=x_raw[:, :, H3_COLS:K], in_=xin[:, :, 0:3])
+            nc.vector.tensor_copy(out=b4g[:], in_=b4r[:].rearrange("p a e -> p (a e)"))
+            done.add("fix")
+            return True
+
+        def op_t(row, eng):
+            if not slot_free(tr_hist, N_TR) or (row[0] == "x" and "fix" not in done):
+                return False
             words = row_src(row).bitcast(F32)
             bank = ps_tr.tile([P, 512], F32, name="tr", tag="tr")
             for c in range(4):
@@ -125,9 +216,16 @@ def tile_implicitnet_pa_kernel(tc, h3, x_in, W4, b4, W5, b5, out):
                     bank[:, c * P : (c + 1) * P], words[:, c * P : (c + 1) * P], ident[:]
                 )
             banks[row] = bank
+            tr_hist.append(row)
+            done.add(("t", row))
+            return True
 
-        def do_e(row):
+        def op_e(row, eng):
+            if ("t", row) not in done:
+                return False
             kind, i = row
+            if kind != "w5" and not slot_free(grp_hist, N_GRP):
+                return False
             src = banks[row][:].rearrange("p (k u r) -> p k r u", k=2, u=2)
             if kind == "w5":
                 dst = (
@@ -140,38 +238,59 @@ def tile_implicitnet_pa_kernel(tc, h3, x_in, W4, b4, W5, b5, out):
             else:
                 g_t = grp_pool.tile([P, K], BF16, name="grp", tag="grp", align_bytes=64)
                 grps[row] = g_t
+                grp_hist.append(("grp", row))
                 dst = g_t[:].bitcast(F32).rearrange("p (k r u) -> p k r u", k=2, u=2)
-            if row in V_EVACS:
+            if eng == "dve":
                 nc.vector.tensor_copy(out=dst, in_=src)
             else:
                 nc.scalar.copy(out=dst, in_=src)
+            done.add(("rel", row))
+            done.add(("e", row))
+            return True
 
-        def do_m(row):
+        def op_m(t, eng):
+            row = ("x", t)
+            if ("e", row) not in done or not slot_free(xsc_hist, N_XSC):
+                return False
             x_t = xsc_pool.tile([P, K], BF16, name="xsc", tag="xsc", align_bytes=64)
             nc.vector.tensor_scalar(
                 out=x_t[:], in0=grps[row][:], scalar1=math.sqrt(0.5), scalar2=None, op0=ALU.mult
             )
             grps[row] = x_t
+            xsc_hist.append(("xsc", row))
+            done.add(("rel", ("grp", row)))
+            done.add(("m", row))
+            return True
 
-        def do_q(row):
-            kind, i = row
+        def op_q(rows, eng):
+            kind = rows[0][0]
+            if not have([("m" if kind == "x" else "e", r) for r in rows]):
+                return False
             if kind == "w5":
-                h = i // 4
+                h = rows[0][1] // 4
                 nc.vector.quantize_mx(
                     out=w5c[:, h * 1024 : (h + 1) * 1024].bitcast(FP8X4),
                     scales=w5s[:, h * 1024 : (h + 1) * 1024],
                     in_=w5g[h][:],
                 )
-                return
-            cd, sc = (xc, xs) if kind == "x" else (w4c, w4s)
-            nc.vector.quantize_mx(
-                out=cd[:, i * 256 : (i + 1) * 256].bitcast(FP8X4),
-                scales=sc[:, i * 256 : (i + 1) * 256],
-                in_=grps[row][:],
-            )
+            else:
+                i = rows[0][1]
+                cd, sc = (xc, xs) if kind == "x" else (w4c, w4s)
+                nc.vector.quantize_mx(
+                    out=cd[:, i * 256 : (i + 1) * 256].bitcast(FP8X4),
+                    scales=sc[:, i * 256 : (i + 1) * 256],
+                    in_=grps[rows[0]][:],
+                )
+            for r in rows:
+                done.add(("q", r))
+                done.add(("rel", ("xsc" if kind == "x" else "grp", r)))
+            return True
 
-        def do_mm1(unit):
+        def op_mm1(unit, eng):
             g, t = unit
+            need = [("q", ("x", t))] + [("q", ("w4", g * 4 + j)) for j in range(4)]
+            if not have(need) or not slot_free(mm_hist, N_MM):
+                return False
             bank = ps_mm.tile([P, 512], F32, name="mm", tag="mm")
             for j in range(4):
                 for kg in range(2):
@@ -186,91 +305,92 @@ def tile_implicitnet_pa_kernel(tc, h3, x_in, W4, b4, W5, b5, out):
                         start=(kg == 0),
                         stop=(kg == 1),
                     )
-            banks[unit] = bank
+            banks[("l1", unit)] = bank
+            mm_hist.append(("l1", unit))
+            done.add(("mm1", unit))
+            return True
 
-        def do_v1(unit):
+        def op_v1(unit, eng):
+            if ("mm1", unit) not in done:
+                return False
             g, t = unit
             nc.vector.tensor_tensor(
-                out=v[t][:, g * 512 : (g + 1) * 512].rearrange("p (w j) -> p w j", j=4),
-                in0=banks[unit][:].rearrange("p (j w) -> p w j", j=4),
+                out=v_all[:, g, t, :].rearrange("p (w j) -> p w j", j=4),
+                in0=banks[("l1", unit)][:].rearrange("p (j w) -> p w j", j=4),
                 in1=b4g[:, g * 4 : (g + 1) * 4].unsqueeze(1).to_broadcast([P, P, 4]),
                 op=ALU.add,
             )
+            done.add(("rel", ("l1", unit)))
+            done.add(("v1", unit))
+            return True
 
-        def do_s1(unit):
-            g, t = unit
+        def sigmoid(units):
             nc.scalar.activation(
-                out=s[t][:, g * 512 : (g + 1) * 512],
-                in_=v[t][:, g * 512 : (g + 1) * 512],
-                func=ACT.Sigmoid,
-                scale=-100.0,
+                out=view(s_all, units), in_=view(v_all, units), func=ACT.Sigmoid, scale=-100.0
             )
 
-        rows = (
-            [("w4", i) for i in range(4)]
-            + [("x", t) for t in range(4)]
-            + [("w4", i) for i in range(4, 8)]
-            + [("x", t) for t in range(4, 8)]
-            + [("w5", r) for r in range(8)]
-        )
-        plan = {}
+        def logarithm(units):
+            nc.scalar.activation(
+                out=view(s_all, units), in_=view(s_all, units), func=ACT.Ln, bias=delta[:, 0:1]
+            )
 
-        def at(step, stage, item):
-            plan[(step, stage)] = plan.get((step, stage), []) + [item]
+        def op_s1(units, eng):
+            if not have([("v1", u) for u in units]):
+                return False
+            sigmoid(units)
+            for u in units:
+                done.add(("s1", u))
+            return True
 
-        q_step = {}
-        for i, row in enumerate(rows):
-            at(i, "t", row)
-            at(i + 1, "e", row)
-            if row[0] == "x":
-                at(i + 2, "m", row)
-                at(i + 3, "q", row)
-                q_step[row] = i + 3
-            elif row[0] == "w4":
-                at(i + 2, "q", row)
-                q_step[row] = i + 2
-            elif row[1] % 4 == 3:
-                at(i + 2, "q", row)
-        last = 0
-        unit_list = (
-            [(0, t) for t in range(4)]
-            + [(1, t) for t in range(4)]
-            + [(g, t) for t in range(4, 8) for g in range(2)]
-        )
-        for unit in unit_list:
-            g, t = unit
-            ready = max(q_step[("x", t)], q_step[("w4", g * 4 + 3)]) + 1
-            at(ready, "mm1", unit)
-            at(ready + 1, "v1", unit)
-            at(ready + 2, "s1", unit)
-            last = max(last, ready + 2)
-        last = max(last, len(rows) + 2)
-        stages = (
-            ("s1", do_s1),
-            ("v1", do_v1),
-            ("mm1", do_mm1),
-            ("q", do_q),
-            ("m", do_m),
-            ("e", do_e),
-            ("t", do_t),
-        )
-        for step in range(last + 1):
-            for stage, fn in stages:
-                for item in plan.get((step, stage), []):
-                    fn(item)
+        def op_ln1(units, eng):
+            if not have([("s1", u) for u in units]):
+                return False
+            logarithm(units)
+            for u in units:
+                done.add(("ln1", u))
+            return True
 
-        def softplus_end(dst, t):
+        def op_f1(units, eng):
+            if not have([("ln1", u) for u in units]) or not slot_free(h4g_hist, N_H4G):
+                return False
+            h_t = h4g_pool.tile([P, K], BF16, name="h4g", tag="h4g", align_bytes=64)
             nc.vector.scalar_tensor_tensor(
-                out=dst, in0=s[t][:], scalar=-0.01, in1=v[t][:], op0=ALU.mult, op1=ALU.max
+                out=h_t[:, 0 : 512 * len(units)],
+                in0=view(s_all, units),
+                scalar=-0.01,
+                in1=view(v_all, units),
+                op0=ALU.mult,
+                op1=ALU.max,
             )
+            grps[units] = h_t
+            h4g_hist.append(("h4g", units))
+            for u in units:
+                done.add(("f1", u))
+            return True
 
-        def do_ln(t):
-            nc.scalar.activation(out=s[t][:], in_=s[t][:], func=ACT.Ln, bias=delta[:, 0:1])
+        def op_q1(units, eng):
+            if not have([("f1", u) for u in units]):
+                return False
+            o = (units[0][0] * NT + units[0][1]) * P
+            n = len(units)
+            nc.vector.quantize_mx(
+                out=h4c[:, o : o + n * P].bitcast(FP8X4),
+                scales=h4s[:, o : o + n * P],
+                in_=grps[units][:, 0 : 512 * n],
+            )
+            done.add(("rel", ("h4g", units)))
+            for u in units:
+                done.add(("q1", u))
+            return True
 
-        def do_mm2(t, hh):
+        def op_mm2(unit, eng):
+            t, hh = unit
+            need = [("q1", (0, t)), ("q1", (1, t))] + [("q", ("w5", hh * 4 + i)) for i in range(4)]
+            if not have(need) or not slot_free(mm_hist, N_MM):
+                return False
             bank = ps_mm.tile([P, 512], F32, name="mm", tag="mm")
             for g in range(2):
-                ho = (t * 2 + g) * P
+                ho = (g * NT + t) * P
                 wo = (hh * 2 + g) * 512
                 nc.tensor.matmul_mx(
                     out=bank[:],
@@ -281,37 +401,77 @@ def tile_implicitnet_pa_kernel(tc, h3, x_in, W4, b4, W5, b5, out):
                     start=(g == 0),
                     stop=(g == 1),
                 )
-            banks[("l2", t, hh)] = bank
+            banks[("l2", unit)] = bank
+            mm_hist.append(("l2", unit))
+            done.add(("mm2", unit))
+            return True
 
-        def do_v2(t, hh):
+        def op_v2(unit, eng):
+            if ("mm2", unit) not in done:
+                return False
+            t, hh = unit
             nc.vector.tensor_tensor(
-                out=v[t][:, hh * 512 : (hh + 1) * 512],
-                in0=banks[("l2", t, hh)][:],
+                out=v_all[:, hh, t, :],
+                in0=banks[("l2", unit)][:],
                 in1=b5bc[:, hh * 512 : (hh + 1) * 512],
                 op=ALU.add,
             )
+            done.add(("rel", ("l2", unit)))
+            done.add(("v2", unit))
+            return True
 
-        for t in range(NT + 2):
-            if t < NT:
-                do_ln(t)
-                h_t = h4g_pool.tile([P, K], BF16, name="h4g", tag="h4g", align_bytes=64)
-                softplus_end(h_t[:], t)
-            if t >= 2:
-                do_v2(t - 2, 0)
-                do_v2(t - 2, 1)
-            if t < NT:
-                nc.vector.quantize_mx(
-                    out=h4c[:, t * 256 : (t + 1) * 256].bitcast(FP8X4),
-                    scales=h4s[:, t * 256 : (t + 1) * 256],
-                    in_=h_t[:],
+        def op_s2(units, eng):
+            if not have([("v2", u) for u in units]):
+                return False
+            sigmoid(l2u(units))
+            for u in units:
+                done.add(("s2", u))
+            return True
+
+        def op_ln2(units, eng):
+            if not have([("s2", u) for u in units]):
+                return False
+            logarithm(l2u(units))
+            for u in units:
+                done.add(("ln2", u))
+            return True
+
+        def op_f2(units, eng):
+            if not have([("ln2", u) for u in units]):
+                return False
+            where = l2u(units)
+            nc.vector.scalar_tensor_tensor(
+                out=view(s_all, where),
+                in0=view(s_all, where),
+                scalar=-0.01,
+                in1=view(v_all, where),
+                op0=ALU.mult,
+                op1=ALU.max,
+            )
+            t = units[0][0]
+            if len(units) == 1:
+                hh = units[0][1]
+                nc.sync.dma_start(
+                    out=out[t * P : (t + 1) * P, hh * 512 : (hh + 1) * 512],
+                    in_=s_all[:, hh, t, :],
                 )
-                do_mm2(t, 0)
-                do_mm2(t, 1)
+            else:
+                nc.sync.dma_start(
+                    out=out[t * P : (t + 1) * P, :].rearrange("p (h c) -> p h c", h=2),
+                    in_=s_all[:, :, t, :],
+                )
+            return True
 
-        for t in range(NT):
-            nc.scalar.activation(out=s[t][:], in_=v[t][:], func=ACT.Sigmoid, scale=-100.0)
-
-        for t in range(NT):
-            do_ln(t)
-            softplus_end(s[t][:], t)
-            nc.sync.dma_start(out=out[t * P : (t + 1) * P, :], in_=s[t][:])
+        ops = {
+            "fix": op_fix, "t": op_t, "e": op_e, "m": op_m, "q": op_q, "mm1": op_mm1,
+            "v1": op_v1, "s1": op_s1, "ln1": op_ln1, "f1": op_f1, "q1": op_q1,
+            "mm2": op_mm2, "v2": op_v2, "s2": op_s2, "ln2": op_ln2, "f2": op_f2,
+        }
+        queues = (("pe", PE_ORDER), ("act", ACT_ORDER), ("dve", DVE_ORDER))
+        pos = [0, 0, 0]
+        total = len(PE_ORDER) + len(ACT_ORDER) + len(DVE_ORDER)
+        for sweep in range(total):
+            for qi, (eng, order) in enumerate(queues):
+                while pos[qi] < len(order) and ops[order[pos[qi]][0]](order[pos[qi]][1], eng):
+                    pos[qi] += 1
+        assert sum(pos) == total

@@ -24,36 +24,36 @@ N_GRP = 10
 N_XSC = 4
 N_H4G = 4
 
-LOADS = ("w4t0", "w4t1", "w4t2", "w4t3", "small", "x0", "x1", "x2", "x3", "x4", "x5", "x6", "x7", "w4t4", "w4t5", "w4t6", "w4t7", "w5c0", "w5c1", "w5c2", "w5c3", "b5")
+LOADS = ("w4t0", "w4t1", "w4t2", "w4t3", "small", "x0", "x1", "x2", "x3", "w4t4", "w4t5", "w4t6", "w4t7", "x4", "x5", "x6", "x7", "w5c0", "w5c1", "w5c2", "w5c3", "b5")
 PE_ORDER = (
     ("t", ("w4", 0)), ("t", ("w4", 1)), ("t", ("w4", 2)), ("t", ("w4", 3)),
-    ("t", ("x", 0)), ("t", ("x", 1)), ("t", ("x", 2)), ("t", ("x", 3)),
-    ("mm1", (0, 0)), ("t", ("x", 4)), ("t", ("x", 5)), ("mm1", (0, 1)),
-    ("t", ("x", 6)), ("mm1", (0, 2)), ("t", ("x", 7)), ("mm1", (0, 3)),
-    ("t", ("w4", 4)), ("mm1", (0, 4)), ("t", ("w4", 5)), ("mm1", (0, 5)),
-    ("t", ("w4", 6)), ("mm1", (0, 6)), ("t", ("w4", 7)), ("mm1", (0, 7)),
-    ("t", ("w5", 0)), ("t", ("w5", 1)), ("t", ("w5", 2)), ("t", ("w5", 3)),
-    ("mm1", (1, 0)), ("mm1", (1, 1)), ("mm1", (1, 2)), ("mm1", (1, 3)),
-    ("mm1", (1, 4)), ("mm1", (1, 5)), ("mm1", (1, 6)), ("mm1", (1, 7)),
-    ("t", ("w5", 4)), ("t", ("w5", 5)), ("t", ("w5", 6)), ("t", ("w5", 7)),
-    ("mm2", (0, 0)), ("mm2", (1, 0)), ("mm2", (2, 0)), ("mm2", (3, 0)),
-    ("mm2", (5, 0)), ("mm2", (4, 0)), ("mm2", (6, 0)), ("mm2", (7, 0)),
-    ("mm2", (0, 1)), ("mm2", (1, 1)), ("mm2", (2, 1)), ("mm2", (3, 1)),
-    ("mm2", (4, 1)), ("mm2", (5, 1)), ("mm2", (6, 1)), ("mm2", (7, 1)),
+    ("t", ("x", 0)), ("t", ("x", 1)), ("t", ("x", 2)), ("mm1", (0, 0)),
+    ("t", ("x", 3)), ("t", ("w4", 4)), ("mm1", (0, 1)), ("t", ("w4", 5)),
+    ("mm1", (0, 2)), ("t", ("w4", 6)), ("mm1", (0, 3)), ("t", ("w4", 7)),
+    ("t", ("x", 4)), ("t", ("x", 6)), ("t", ("x", 5)), ("mm1", (1, 0)),
+    ("mm1", (1, 1)), ("t", ("x", 7)), ("mm1", (1, 3)), ("mm1", (1, 2)),
+    ("t", ("w5", 1)), ("t", ("w5", 0)), ("mm1", (0, 4)), ("mm1", (0, 5)),
+    ("t", ("w5", 2)), ("t", ("w5", 3)), ("mm1", (1, 4)), ("mm1", (1, 5)),
+    ("mm1", (0, 6)), ("mm1", (1, 6)), ("mm1", (0, 7)), ("t", ("w5", 4)),
+    ("mm1", (1, 7)), ("t", ("w5", 5)), ("t", ("w5", 6)), ("t", ("w5", 7)),
+    ("mm2", (0, 0)), ("mm2", (0, 1)), ("mm2", (1, 0)), ("mm2", (1, 1)),
+    ("mm2", (2, 0)), ("mm2", (2, 1)), ("mm2", (3, 0)), ("mm2", (3, 1)),
+    ("mm2", (4, 0)), ("mm2", (4, 1)), ("mm2", (5, 0)), ("mm2", (5, 1)),
+    ("mm2", (6, 0)), ("mm2", (6, 1)), ("mm2", (7, 0)), ("mm2", (7, 1)),
 )
 ACT_ORDER = (
     ("e", ("w4", 0)), ("e", ("w4", 1)), ("e", ("w4", 2)), ("e", ("w4", 3)),
-    ("e", ("x", 1)), ("e", ("x", 2)), ("e", ("x", 3)), ("e", ("x", 4)),
-    ("e", ("x", 5)), ("e", ("x", 6)), ("e", ("x", 7)), ("e", ("w4", 4)),
-    ("e", ("w4", 5)), ("e", ("w4", 6)), ("s1", ((0, 0), (0, 1),)), ("e", ("w4", 7)),
-    ("s1", ((0, 2), (0, 3),)), ("s1", ((0, 4), (0, 5),)), ("s1", ((0, 6), (0, 7),)), ("s1", ((1, 0), (1, 1),)),
-    ("s1", ((1, 2), (1, 3),)), ("s1", ((1, 4), (1, 5),)), ("s1", ((1, 6), (1, 7),)), ("ln1", ((0, 0), (0, 1),)),
-    ("ln1", ((1, 0), (1, 1),)), ("ln1", ((0, 2), (0, 3),)), ("ln1", ((1, 2), (1, 3),)), ("ln1", ((0, 4), (0, 5),)),
-    ("ln1", ((1, 4), (1, 5),)), ("ln1", ((0, 6), (0, 7),)), ("ln1", ((1, 6), (1, 7),)), ("e", ("w5", 4)),
-    ("e", ("w5", 5)), ("e", ("w5", 6)), ("e", ("w5", 7)), ("s2", ((0, 0), (1, 0),)),
-    ("s2", ((2, 0), (3, 0),)), ("s2", ((4, 0), (5, 0),)), ("s2", ((6, 0), (7, 0),)), ("s2", ((0, 1), (1, 1),)),
-    ("s2", ((2, 1), (3, 1),)), ("s2", ((4, 1), (5, 1),)), ("s2", ((6, 1), (7, 1),)), ("ln2", ((0, 0),)),
-    ("ln2", ((0, 1),)), ("ln2", ((1, 0), (1, 1),)), ("ln2", ((2, 0), (2, 1),)), ("ln2", ((3, 0), (3, 1),)),
+    ("e", ("x", 1)), ("e", ("x", 2)), ("e", ("x", 3)), ("e", ("w4", 4)),
+    ("e", ("w4", 5)), ("e", ("w4", 6)), ("e", ("w4", 7)), ("s1", ((0, 2), (0, 3),)),
+    ("e", ("x", 6)), ("e", ("x", 5)), ("s1", ((0, 0), (0, 1),)), ("e", ("x", 7)),
+    ("s1", ((1, 0), (1, 1),)), ("e", ("w5", 1)), ("s1", ((1, 2), (1, 3),)), ("ln1", ((0, 0), (0, 1),)),
+    ("e", ("w5", 3)), ("ln1", ((1, 0), (1, 1),)), ("ln1", ((0, 2), (0, 3),)), ("ln1", ((1, 2), (1, 3),)),
+    ("e", ("w5", 4)), ("e", ("w5", 5)), ("e", ("w5", 6)), ("e", ("w5", 7)),
+    ("s1", ((0, 4), (1, 4),)), ("s1", ((0, 5), (1, 5),)), ("s1", ((0, 6), (1, 6),)), ("s1", ((0, 7), (1, 7),)),
+    ("s2", ((0, 0), (0, 1),)), ("s2", ((1, 0), (1, 1),)), ("s2", ((2, 0), (2, 1),)), ("s2", ((3, 0), (3, 1),)),
+    ("ln1", ((0, 4), (0, 5),)), ("ln1", ((1, 4), (1, 5),)), ("ln1", ((0, 6), (0, 7),)), ("ln1", ((1, 6), (1, 7),)),
+    ("ln2", ((0, 0), (0, 1),)), ("ln2", ((1, 0), (1, 1),)), ("ln2", ((2, 0), (2, 1),)), ("ln2", ((3, 0), (3, 1),)),
+    ("s2", ((4, 0), (4, 1),)), ("s2", ((5, 0), (5, 1),)), ("s2", ((6, 0), (6, 1),)), ("s2", ((7, 0), (7, 1),)),
     ("ln2", ((4, 0), (4, 1),)), ("ln2", ((5, 0), (5, 1),)), ("ln2", ((6, 0), (6, 1),)), ("ln2", ((7, 0),)),
     ("ln2", ((7, 1),)),
 )
@@ -61,26 +61,25 @@ DVE_ORDER = (
     ("q", (("w4", 0),)), ("q", (("w4", 1),)), ("fix", 0), ("q", (("w4", 2),)),
     ("q", (("w4", 3),)), ("e", ("x", 0)), ("m", 0), ("q", (("x", 0),)),
     ("m", 1), ("q", (("x", 1),)), ("m", 2), ("q", (("x", 2),)),
-    ("m", 3), ("v1", (0, 0)), ("m", 4), ("q", (("x", 3),)),
-    ("v1", (0, 1)), ("m", 5), ("q", (("x", 4),)), ("v1", (0, 2)),
-    ("m", 6), ("q", (("x", 5),)), ("v1", (0, 3)), ("m", 7),
-    ("q", (("x", 6),)), ("v1", (0, 4)), ("q", (("x", 7),)), ("q", (("w4", 4),)),
-    ("q", (("w4", 5),)), ("q", (("w4", 6),)), ("v1", (0, 7)), ("q", (("w4", 7),)),
-    ("v1", (0, 5)), ("v1", (0, 6)), ("v1", (1, 0)), ("v1", (1, 1)),
-    ("v1", (1, 2)), ("v1", (1, 3)), ("v1", (1, 4)), ("v1", (1, 5)),
-    ("v1", (1, 6)), ("v1", (1, 7)), ("e", ("w5", 0)), ("e", ("w5", 1)),
-    ("e", ("w5", 2)), ("e", ("w5", 3)), ("q", (("w5", 0), ("w5", 1), ("w5", 2), ("w5", 3),)), ("f1", ((0, 0), (0, 1),)),
-    ("f1", ((1, 0), (1, 1),)), ("q1", ((0, 0), (0, 1),)), ("q1", ((1, 0), (1, 1),)), ("f1", ((0, 2), (0, 3),)),
-    ("f1", ((1, 2), (1, 3),)), ("v2", (0, 0)), ("v2", (1, 0)), ("q1", ((0, 2), (0, 3),)),
-    ("q1", ((1, 2), (1, 3),)), ("f1", ((0, 4), (0, 5),)), ("f1", ((1, 4), (1, 5),)), ("v2", (2, 0)),
-    ("v2", (3, 0)), ("q1", ((0, 4), (0, 5),)), ("q1", ((1, 4), (1, 5),)), ("f1", ((0, 6), (0, 7),)),
-    ("f1", ((1, 6), (1, 7),)), ("v2", (5, 0)), ("q1", ((0, 6), (0, 7),)), ("q1", ((1, 6), (1, 7),)),
-    ("q", (("w5", 4), ("w5", 5), ("w5", 6), ("w5", 7),)), ("v2", (4, 0)), ("v2", (7, 0)), ("v2", (6, 0)),
-    ("v2", (0, 1)), ("v2", (1, 1)), ("v2", (2, 1)), ("v2", (3, 1)),
-    ("v2", (4, 1)), ("v2", (5, 1)), ("v2", (6, 1)), ("v2", (7, 1)),
-    ("f2", ((0, 0),)), ("f2", ((0, 1),)), ("f2", ((1, 0), (1, 1),)), ("f2", ((2, 0), (2, 1),)),
-    ("f2", ((3, 0), (3, 1),)), ("f2", ((4, 0), (4, 1),)), ("f2", ((5, 0), (5, 1),)), ("f2", ((6, 0), (6, 1),)),
-    ("f2", ((7, 0),)), ("f2", ((7, 1),)),
+    ("v1", (0, 0)), ("m", 3), ("v1", (0, 1)), ("q", (("x", 3),)),
+    ("v1", (0, 2)), ("q", (("w4", 4),)), ("q", (("w4", 5),)), ("v1", (0, 3)),
+    ("q", (("w4", 6),)), ("q", (("w4", 7),)), ("e", ("x", 4)), ("m", 4),
+    ("v1", (1, 0)), ("q", (("x", 4),)), ("m", 5), ("v1", (1, 1)),
+    ("q", (("x", 5),)), ("m", 6), ("v1", (1, 3)), ("v1", (1, 2)),
+    ("m", 7), ("q", (("x", 6),)), ("e", ("w5", 0)), ("q", (("x", 7),)),
+    ("v1", (0, 4)), ("v1", (0, 5)), ("e", ("w5", 2)), ("v1", (1, 4)),
+    ("v1", (1, 5)), ("v1", (0, 6)), ("v1", (1, 6)), ("q", (("w5", 0), ("w5", 1), ("w5", 2), ("w5", 3),)),
+    ("v1", (0, 7)), ("v1", (1, 7)), ("f1", ((0, 0), (0, 1),)), ("f1", ((1, 0), (1, 1),)),
+    ("q1", ((0, 0), (0, 1),)), ("q1", ((1, 0), (1, 1),)), ("q", (("w5", 4), ("w5", 5), ("w5", 6), ("w5", 7),)), ("f1", ((0, 2), (0, 3),)),
+    ("f1", ((1, 2), (1, 3),)), ("q1", ((0, 2), (0, 3),)), ("q1", ((1, 2), (1, 3),)), ("v2", (0, 0)),
+    ("v2", (0, 1)), ("v2", (1, 0)), ("v2", (1, 1)), ("v2", (2, 0)),
+    ("v2", (2, 1)), ("v2", (3, 0)), ("v2", (3, 1)), ("f1", ((0, 4), (0, 5),)),
+    ("f1", ((1, 4), (1, 5),)), ("q1", ((0, 4), (0, 5),)), ("q1", ((1, 4), (1, 5),)), ("f1", ((0, 6), (0, 7),)),
+    ("f1", ((1, 6), (1, 7),)), ("q1", ((0, 6), (0, 7),)), ("q1", ((1, 6), (1, 7),)), ("v2", (4, 0)),
+    ("v2", (4, 1)), ("f2", ((0, 0), (0, 1),)), ("v2", (5, 0)), ("v2", (5, 1)),
+    ("v2", (6, 0)), ("v2", (6, 1)), ("v2", (7, 0)), ("v2", (7, 1)),
+    ("f2", ((2, 0), (2, 1),)), ("f2", ((1, 0), (1, 1),)), ("f2", ((3, 0), (3, 1),)), ("f2", ((4, 0), (4, 1),)),
+    ("f2", ((5, 0), (5, 1),)), ("f2", ((6, 0), (6, 1),)), ("f2", ((7, 0),)), ("f2", ((7, 1),)),
 )
 
 

@@ -12,465 +12,295 @@ FP8X4 = mybir.dt.float8_e4m3fn_x4
 ACT = mybir.ActivationFunctionType
 ALU = mybir.AluOpType
 
+FLOPS = 2 * 2 * 1024 * 1024 * 1024
+
 P = 128
 K = 1024
-H3_COLS = 1021
-DMA_COLS = 1008
 NT = 8
-FLOPS = 2 * 2 * 1024 * 1024 * 1024
-N_TR = 4
-N_MM = 4
-N_GRP = 10
-N_XSC = 4
-N_H4G = 4
+UNIT = 512
+H3_COLS = 1021
+WHOLE_BLOCKS = 1008
+LN_FLOOR = 2.0 ** -60
 
-LOADS = ("w4t0", "w4t1", "w4t2", "w4t3", "small", "x0", "x1", "x2", "x3", "w4t4", "w4t5", "w4t6", "w4t7", "x4", "x5", "x6", "x7", "w5c0", "w5c1", "w5c2", "w5c3", "b5")
-PE_ORDER = (
-    ("t", ("w4", 0)), ("t", ("w4", 1)), ("t", ("w4", 2)), ("t", ("w4", 3)),
-    ("t", ("x", 0)), ("t", ("x", 1)), ("t", ("x", 2)), ("mm1", (0, 0)),
-    ("t", ("x", 3)), ("t", ("w4", 4)), ("mm1", (0, 1)), ("t", ("w4", 5)),
-    ("mm1", (0, 2)), ("t", ("w4", 6)), ("mm1", (0, 3)), ("t", ("w4", 7)),
-    ("t", ("x", 4)), ("t", ("x", 6)), ("t", ("x", 5)), ("mm1", (1, 0)),
-    ("mm1", (1, 1)), ("t", ("x", 7)), ("mm1", (1, 3)), ("mm1", (1, 2)),
-    ("t", ("w5", 1)), ("t", ("w5", 0)), ("mm1", (0, 4)), ("mm1", (0, 5)),
-    ("t", ("w5", 2)), ("t", ("w5", 3)), ("mm1", (1, 4)), ("mm1", (1, 5)),
-    ("mm1", (0, 6)), ("mm1", (1, 6)), ("mm1", (0, 7)), ("t", ("w5", 4)),
-    ("mm1", (1, 7)), ("t", ("w5", 5)), ("t", ("w5", 6)), ("t", ("w5", 7)),
-    ("mm2", (0, 0)), ("mm2", (0, 1)), ("mm2", (1, 0)), ("mm2", (1, 1)),
-    ("mm2", (2, 0)), ("mm2", (2, 1)), ("mm2", (3, 0)), ("mm2", (3, 1)),
-    ("mm2", (4, 0)), ("mm2", (4, 1)), ("mm2", (5, 0)), ("mm2", (5, 1)),
-    ("mm2", (6, 0)), ("mm2", (6, 1)), ("mm2", (7, 0)), ("mm2", (7, 1)),
-)
-ACT_ORDER = (
-    ("e", ("w4", 0)), ("e", ("w4", 1)), ("e", ("w4", 2)), ("e", ("w4", 3)),
-    ("e", ("x", 1)), ("e", ("x", 2)), ("e", ("x", 3)), ("e", ("w4", 4)),
-    ("e", ("w4", 5)), ("e", ("w4", 6)), ("e", ("w4", 7)), ("s1", ((0, 2), (0, 3),)),
-    ("e", ("x", 6)), ("e", ("x", 5)), ("s1", ((0, 0), (0, 1),)), ("e", ("x", 7)),
-    ("s1", ((1, 0), (1, 1),)), ("e", ("w5", 1)), ("s1", ((1, 2), (1, 3),)), ("ln1", ((0, 0), (0, 1),)),
-    ("e", ("w5", 3)), ("ln1", ((1, 0), (1, 1),)), ("ln1", ((0, 2), (0, 3),)), ("ln1", ((1, 2), (1, 3),)),
-    ("e", ("w5", 4)), ("e", ("w5", 5)), ("e", ("w5", 6)), ("e", ("w5", 7)),
-    ("s1", ((0, 4), (1, 4),)), ("s1", ((0, 5), (1, 5),)), ("s1", ((0, 6), (1, 6),)), ("s1", ((0, 7), (1, 7),)),
-    ("s2", ((0, 0), (0, 1),)), ("s2", ((1, 0), (1, 1),)), ("s2", ((2, 0), (2, 1),)), ("s2", ((3, 0), (3, 1),)),
-    ("ln1", ((0, 4), (0, 5),)), ("ln1", ((1, 4), (1, 5),)), ("ln1", ((0, 6), (0, 7),)), ("ln1", ((1, 6), (1, 7),)),
-    ("ln2", ((0, 0), (0, 1),)), ("ln2", ((1, 0), (1, 1),)), ("ln2", ((2, 0), (2, 1),)), ("ln2", ((3, 0), (3, 1),)),
-    ("s2", ((4, 0), (4, 1),)), ("s2", ((5, 0), (5, 1),)), ("s2", ((6, 0), (6, 1),)), ("s2", ((7, 0), (7, 1),)),
-    ("ln2", ((4, 0), (4, 1),)), ("ln2", ((5, 0), (5, 1),)), ("ln2", ((6, 0), (6, 1),)), ("ln2", ((7, 0),)),
-    ("ln2", ((7, 1),)),
-)
-DVE_ORDER = (
-    ("q", (("w4", 0),)), ("q", (("w4", 1),)), ("fix", 0), ("q", (("w4", 2),)),
-    ("q", (("w4", 3),)), ("e", ("x", 0)), ("m", 0), ("q", (("x", 0),)),
-    ("m", 1), ("q", (("x", 1),)), ("m", 2), ("q", (("x", 2),)),
-    ("v1", (0, 0)), ("m", 3), ("v1", (0, 1)), ("q", (("x", 3),)),
-    ("v1", (0, 2)), ("q", (("w4", 4),)), ("q", (("w4", 5),)), ("v1", (0, 3)),
-    ("q", (("w4", 6),)), ("q", (("w4", 7),)), ("e", ("x", 4)), ("m", 4),
-    ("v1", (1, 0)), ("q", (("x", 4),)), ("m", 5), ("v1", (1, 1)),
-    ("q", (("x", 5),)), ("m", 6), ("v1", (1, 3)), ("v1", (1, 2)),
-    ("m", 7), ("q", (("x", 6),)), ("e", ("w5", 0)), ("q", (("x", 7),)),
-    ("v1", (0, 4)), ("v1", (0, 5)), ("e", ("w5", 2)), ("v1", (1, 4)),
-    ("v1", (1, 5)), ("v1", (0, 6)), ("v1", (1, 6)), ("q", (("w5", 0), ("w5", 1), ("w5", 2), ("w5", 3),)),
-    ("v1", (0, 7)), ("v1", (1, 7)), ("f1", ((0, 0), (0, 1),)), ("f1", ((1, 0), (1, 1),)),
-    ("q1", ((0, 0), (0, 1),)), ("q1", ((1, 0), (1, 1),)), ("q", (("w5", 4), ("w5", 5), ("w5", 6), ("w5", 7),)), ("f1", ((0, 2), (0, 3),)),
-    ("f1", ((1, 2), (1, 3),)), ("q1", ((0, 2), (0, 3),)), ("q1", ((1, 2), (1, 3),)), ("v2", (0, 0)),
-    ("v2", (0, 1)), ("v2", (1, 0)), ("v2", (1, 1)), ("v2", (2, 0)),
-    ("v2", (2, 1)), ("v2", (3, 0)), ("v2", (3, 1)), ("f1", ((0, 4), (0, 5),)),
-    ("f1", ((1, 4), (1, 5),)), ("q1", ((0, 4), (0, 5),)), ("q1", ((1, 4), (1, 5),)), ("f1", ((0, 6), (0, 7),)),
-    ("f1", ((1, 6), (1, 7),)), ("q1", ((0, 6), (0, 7),)), ("q1", ((1, 6), (1, 7),)), ("v2", (4, 0)),
-    ("v2", (4, 1)), ("f2", ((0, 0), (0, 1),)), ("v2", (5, 0)), ("v2", (5, 1)),
-    ("v2", (6, 0)), ("v2", (6, 1)), ("v2", (7, 0)), ("v2", (7, 1)),
-    ("f2", ((2, 0), (2, 1),)), ("f2", ((1, 0), (1, 1),)), ("f2", ((3, 0), (3, 1),)), ("f2", ((4, 0), (4, 1),)),
-    ("f2", ((5, 0), (5, 1),)), ("f2", ((6, 0), (6, 1),)), ("f2", ((7, 0),)), ("f2", ((7, 1),)),
-)
+LAG_COPY = 1
+LAG_SCALE = 2
+LAG_QUANTISE = 3
+LAG_MATMUL = 4
+LAG_BIAS = 6
+LAG_SIGMOID = 8
+N_ROWS = 16
+FIRST_X = 4
 
 
 def tile_implicitnet_pa_kernel(tc, h3, x_in, W4, b4, W5, b5, out):
     nc = tc.nc
     with ExitStack() as ctx:
-        const = ctx.enter_context(tc.tile_pool(name="const", bufs=1))
-        raw = ctx.enter_context(tc.tile_pool(name="raw", bufs=1))
-        codes = ctx.enter_context(tc.tile_pool(name="codes", bufs=1))
-        grp_pool = ctx.enter_context(tc.tile_pool(name="grp", bufs=N_GRP))
-        xsc_pool = ctx.enter_context(tc.tile_pool(name="xsc", bufs=N_XSC))
-        h4g_pool = ctx.enter_context(tc.tile_pool(name="h4g", bufs=N_H4G))
-        act = ctx.enter_context(tc.tile_pool(name="act", bufs=1))
-        ps_tr = ctx.enter_context(tc.psum_pool(name="ps_tr", bufs=N_TR))
-        ps_mm = ctx.enter_context(tc.psum_pool(name="ps_mm", bufs=N_MM))
+        keep = ctx.enter_context(tc.tile_pool(name="keep", bufs=1))
+        grouped_pool = ctx.enter_context(tc.tile_pool(name="grouped", bufs=6))
+        scaled_pool = ctx.enter_context(tc.tile_pool(name="scaled", bufs=4))
+        h4_pool = ctx.enter_context(tc.tile_pool(name="h4", bufs=4))
+        tr_pool = ctx.enter_context(tc.psum_pool(name="tr", bufs=4))
+        mm_pool = ctx.enter_context(tc.psum_pool(name="mm", bufs=4))
 
-        ident = const.tile([P, P], F32, name="ident")
+        ident = keep.tile([P, P], F32, name="ident")
         make_identity(nc, ident[:])
 
         ctx.enter_context(tc.manual_schedule())
 
-        x_raw = raw.tile([P, NT, K], BF16, name="x_raw")
-        tail = raw.tile([P, NT, 16], BF16, name="tail")
-        xin = raw.tile([P, NT, 4], BF16, name="xin")
-        w4_raw = raw.tile([P, 4, 2, K], BF16, name="w4_raw")
-        w5_raw = raw.tile([P, NT, K], BF16, name="w5_raw")
-        b4r = const.tile([P, 4, 2], BF16, name="b4r")
-        b4g = const.tile([P, 8], F32, name="b4g")
-        b5bc = const.tile([P, K], BF16, name="b5bc")
-        delta = const.tile([P, 1], F32, name="delta")
-        warm = const.tile([P, 1], F32, name="warm")
+        x_raw = keep.tile([P, NT, K], BF16, name="x_raw")
+        h3_tail = keep.tile([P, NT, 16], BF16, name="h3_tail")
+        xin_sb = keep.tile([P, NT, 4], BF16, name="xin_sb")
+        w4_raw = keep.tile([P, NT, K], BF16, name="w4_raw")
+        w5_raw = keep.tile([P, NT, K], BF16, name="w5_raw")
+        b4_bf = keep.tile([P, NT], BF16, name="b4_bf")
+        b4_f32 = keep.tile([P, NT], F32, name="b4_f32")
+        b5_all = keep.tile([P, K], BF16, name="b5_all")
+        ln_floor = keep.tile([P, 1], F32, name="ln_floor")
+        warm = keep.tile([P, 1], F32, name="warm")
 
-        xc = codes.tile([P, NT * 256], U32, name="xc", align_bytes=64)
-        xs = codes.tile([P, NT * 256], U8, name="xs", align_bytes=64)
-        w4c = codes.tile([P, NT * 256], U32, name="w4c", align_bytes=64)
-        w4s = codes.tile([P, NT * 256], U8, name="w4s", align_bytes=64)
-        w5c = codes.tile([P, 2048], U32, name="w5c", align_bytes=64)
-        w5s = codes.tile([P, 2048], U8, name="w5s", align_bytes=64)
-        h4c = codes.tile([P, 16 * P], U32, name="h4c", align_bytes=64)
-        h4s = codes.tile([P, 16 * P], U8, name="h4s", align_bytes=64)
-        w5g = [
-            raw.tile([P, 4096], BF16, name="w5g%d" % h, align_bytes=64) for h in range(2)
+        x_codes = keep.tile([P, NT * 256], U32, name="x_codes", align_bytes=64)
+        x_scales = keep.tile([P, NT * 256], U8, name="x_scales", align_bytes=64)
+        w4_codes = keep.tile([P, NT * 256], U32, name="w4_codes", align_bytes=64)
+        w4_scales = keep.tile([P, NT * 256], U8, name="w4_scales", align_bytes=64)
+        h4_codes = keep.tile([P, 2 * NT * P], U32, name="h4_codes", align_bytes=64)
+        h4_scales = keep.tile([P, 2 * NT * P], U8, name="h4_scales", align_bytes=64)
+        w5_codes = keep.tile([P, 4 * UNIT], U32, name="w5_codes", align_bytes=64)
+        w5_scales = keep.tile([P, 4 * UNIT], U8, name="w5_scales", align_bytes=64)
+        w5_grouped = [
+            keep.tile([P, 4 * K], BF16, name="w5_grouped%d" % a, align_bytes=64) for a in range(2)
         ]
-        v_all = act.tile([P, 2, NT, 512], F32, name="v_all")
-        s_all = act.tile([P, 2, NT, 512], F32, name="s_all")
+        v_all = keep.tile([P, 2, NT, UNIT], F32, name="v_all")
+        s_all = keep.tile([P, 2, NT, UNIT], F32, name="s_all")
 
-        for name in LOADS:
-            if name == "small":
-                nc.sync.dma_start(
-                    out=tail[:, :, 0:13],
-                    in_=h3[:, DMA_COLS:H3_COLS].rearrange("(t p) c -> p t c", p=P),
-                )
-                nc.sync.dma_start(
-                    out=xin[:, :, 0:3], in_=x_in.rearrange("(t p) c -> p t c", p=P)
-                )
-                nc.sync.dma_start(
-                    out=b4r[:], in_=b4.rearrange("(a p e) -> p a e", a=4, p=P, e=2)
-                )
-            elif name == "b5":
-                nc.sync.dma_start(out=b5bc[:], in_=b5.partition_broadcast(P))
-            elif name[0:3] == "w4t":
-                i = int(name[3:])
-                nc.sync.dma_start(
-                    out=w4_raw[:, i // 2, i % 2, :],
-                    in_=W4[(i // 2) * 256 : (i // 2 + 1) * 256, :].rearrange(
-                        "(p e) k -> p e k", e=2
-                    )[:, i % 2, :],
-                )
-            elif name[0:3] == "w5c":
-                c = int(name[3:])
-                nc.sync.dma_start(
-                    out=w5_raw[:, 2 * c : 2 * c + 2, :],
-                    in_=W5[c * 256 : (c + 1) * 256, :].rearrange("(t p) k -> p t k", p=P),
-                )
-            else:
-                t = int(name[1:])
-                nc.sync.dma_start(
-                    out=x_raw[:, t, 0:DMA_COLS], in_=h3[t * P : (t + 1) * P, 0:DMA_COLS]
-                )
+        def load_w4(i):
+            pair = W4[(i // 2) * 256 : (i // 2 + 1) * 256, :].rearrange("(p e) k -> p e k", e=2)
+            nc.sync.dma_start(out=w4_raw[:, i, :], in_=pair[:, i % 2, :])
+
+        for i in range(4):
+            load_w4(i)
+        nc.sync.dma_start(
+            out=h3_tail[:, :, 0 : H3_COLS - WHOLE_BLOCKS],
+            in_=h3[:, WHOLE_BLOCKS:H3_COLS].rearrange("(t p) c -> p t c", p=P),
+        )
+        nc.sync.dma_start(out=xin_sb[:, :, 0:3], in_=x_in.rearrange("(t p) c -> p t c", p=P))
+        nc.sync.dma_start(
+            out=b4_bf[:].rearrange("p (a e) -> p a e", e=2),
+            in_=b4.rearrange("(a p e) -> p a e", p=P, e=2),
+        )
+        for t in range(NT):
+            nc.sync.dma_start(
+                out=x_raw[:, t, 0:WHOLE_BLOCKS], in_=h3[t * P : (t + 1) * P, 0:WHOLE_BLOCKS]
+            )
+        for i in range(4, NT):
+            load_w4(i)
+        for i in range(0, NT, 2):
+            nc.sync.dma_start(
+                out=w5_raw[:, i : i + 2, :],
+                in_=W5[i * P : (i + 2) * P, :].rearrange("(t p) k -> p t k", p=P),
+            )
+        nc.sync.dma_start(out=b5_all[:], in_=b5.partition_broadcast(P))
 
         nc.vector.memset(warm[:], 0.0)
-        nc.vector.memset(delta[:], 2.0 ** -60)
+        nc.vector.memset(ln_floor[:], LN_FLOOR)
         nc.scalar.activation(out=warm[:], in_=warm[:], func=ACT.Sigmoid)
 
-        done = set()
-        banks = {}
-        grps = {}
-        tr_hist = []
-        mm_hist = []
-        grp_hist = []
-        xsc_hist = []
-        h4g_hist = []
+        def transpose_rows(rows):
+            words = rows.bitcast(F32)
+            bank = tr_pool.tile([P, UNIT], F32, name="tr_bank", tag="tr_bank")
+            for cu in range(4):
+                cols = slice(cu * P, (cu + 1) * P)
+                nc.tensor.transpose(bank[:, cols], words[:, cols], ident[:])
+            return bank
 
-        def have(keys):
-            return all(k in done for k in keys)
+        def bank_words(bank):
+            return bank[:].rearrange("p (c u r) -> p c r u", c=2, u=2)
 
-        def slot_free(hist, depth):
-            return len(hist) < depth or ("rel", hist[len(hist) - depth]) in done
-
-        def view(big, units):
-            if len(units) == 1:
-                return big[:, units[0][0], units[0][1], :]
-            if units[0][0] == units[1][0]:
-                a = units[0][0]
-                return big[:, a, units[0][1] : units[-1][1] + 1, :].rearrange("p t c -> p (t c)")
-            return big[:, :, units[0][1], :]
-
-        def l2u(units):
-            return tuple((hh, t) for (t, hh) in units)
-
-        def row_src(row):
-            kind, i = row
-            if kind == "x":
-                return x_raw[:, i, :]
-            if kind == "w4":
-                return w4_raw[:, i // 2, i % 2, :]
-            return w5_raw[:, i, :]
-
-        def op_fix(arg, eng):
-            nc.vector.tensor_copy(out=x_raw[:, :, DMA_COLS:H3_COLS], in_=tail[:, :, 0:13])
-            nc.vector.tensor_copy(out=x_raw[:, :, H3_COLS:K], in_=xin[:, :, 0:3])
-            nc.vector.tensor_copy(out=b4g[:], in_=b4r[:].rearrange("p a e -> p (a e)"))
-            done.add("fix")
-            return True
-
-        def op_t(row, eng):
-            if not slot_free(tr_hist, N_TR) or (row[0] == "x" and "fix" not in done):
-                return False
-            words = row_src(row).bitcast(F32)
-            bank = ps_tr.tile([P, 512], F32, name="tr", tag="tr")
-            for c in range(4):
-                nc.tensor.transpose(
-                    bank[:, c * P : (c + 1) * P], words[:, c * P : (c + 1) * P], ident[:]
-                )
-            banks[row] = bank
-            tr_hist.append(row)
-            done.add(("t", row))
-            return True
-
-        def op_e(row, eng):
-            if ("t", row) not in done:
-                return False
-            kind, i = row
-            if kind != "w5" and not slot_free(grp_hist, N_GRP):
-                return False
-            src = banks[row][:].rearrange("p (k u r) -> p k r u", k=2, u=2)
-            if kind == "w5":
-                dst = (
-                    w5g[i // 4][:]
-                    .bitcast(F32)
-                    .rearrange("p (g c u) -> p g c u", g=2, u=2)[
-                        :, :, (i % 4) * P : (i % 4 + 1) * P, :
-                    ]
-                )
-            else:
-                g_t = grp_pool.tile([P, K], BF16, name="grp", tag="grp", align_bytes=64)
-                grps[row] = g_t
-                grp_hist.append(("grp", row))
-                dst = g_t[:].bitcast(F32).rearrange("p (k r u) -> p k r u", k=2, u=2)
-            if eng == "dve":
-                nc.vector.tensor_copy(out=dst, in_=src)
-            else:
-                nc.scalar.copy(out=dst, in_=src)
-            done.add(("rel", row))
-            done.add(("e", row))
-            return True
-
-        def op_m(t, eng):
-            row = ("x", t)
-            if ("e", row) not in done or not slot_free(xsc_hist, N_XSC):
-                return False
-            x_t = xsc_pool.tile([P, K], BF16, name="xsc", tag="xsc", align_bytes=64)
-            nc.vector.tensor_scalar(
-                out=x_t[:], in0=grps[row][:], scalar1=math.sqrt(0.5), scalar2=None, op0=ALU.mult
+        def quantise(codes, scales, first, width, values):
+            nc.vector.quantize_mx(
+                out=codes[:, first : first + width].bitcast(FP8X4),
+                scales=scales[:, first : first + width],
+                in_=values,
             )
-            grps[row] = x_t
-            xsc_hist.append(("xsc", row))
-            done.add(("rel", ("grp", row)))
-            done.add(("m", row))
-            return True
 
-        def op_q(rows, eng):
-            kind = rows[0][0]
-            if not have([("m" if kind == "x" else "e", r) for r in rows]):
-                return False
-            if kind == "w5":
-                h = rows[0][1] // 4
-                nc.vector.quantize_mx(
-                    out=w5c[:, h * 1024 : (h + 1) * 1024].bitcast(FP8X4),
-                    scales=w5s[:, h * 1024 : (h + 1) * 1024],
-                    in_=w5g[h][:],
+        def product(bank_cols, lhs, lhs_first, rhs, rhs_first, width, c):
+            nc.tensor.matmul_mx(
+                out=bank_cols,
+                lhsT=lhs[0][:, lhs_first : lhs_first + P].bitcast(FP8X4),
+                lhsT_scale=lhs[1][:, lhs_first : lhs_first + P],
+                rhs=rhs[0][:, rhs_first : rhs_first + width].bitcast(FP8X4),
+                rhs_scale=rhs[1][:, rhs_first : rhs_first + width],
+                start=(c == 0),
+                stop=(c == 1),
+            )
+
+        def sigmoid(a, t):
+            nc.scalar.activation(
+                out=s_all[:, a, t, :], in_=v_all[:, a, t, :], func=ACT.Sigmoid, scale=-100.0
+            )
+
+        def logarithm(cells):
+            nc.scalar.activation(out=cells, in_=cells, func=ACT.Ln, bias=ln_floor[:, 0:1])
+
+        def softplus_end(dst, logs, pre):
+            nc.vector.scalar_tensor_tensor(
+                out=dst, in0=logs, scalar=-0.01, in1=pre, op0=ALU.mult, op1=ALU.max
+            )
+
+        def row_tile(i):
+            if i < FIRST_X:
+                return "w4", i, w4_raw[:, i, :]
+            if i < FIRST_X + NT:
+                return "x", i - FIRST_X, x_raw[:, i - FIRST_X, :]
+            if i < N_ROWS:
+                return "w4", i - NT, w4_raw[:, i - NT, :]
+            return "w5", i - N_ROWS, w5_raw[:, i - N_ROWS, :]
+
+        tr_banks = {}
+        mm_banks = {}
+        grouped = {}
+
+        def copy_row(i):
+            tile_i = grouped_pool.tile([P, K], BF16, name="grouped", tag="grouped", align_bytes=64)
+            nc.scalar.copy(
+                out=tile_i[:].bitcast(F32).rearrange("p (c r u) -> p c r u", c=2, u=2),
+                in_=bank_words(tr_banks[i]),
+            )
+            grouped[i] = tile_i
+
+        def scale_row(i):
+            if row_tile(i)[0] == "x":
+                tile_i = scaled_pool.tile([P, K], BF16, name="scaled", tag="scaled", align_bytes=64)
+                nc.vector.tensor_scalar(
+                    out=tile_i[:],
+                    in0=grouped[i][:],
+                    scalar1=math.sqrt(0.5),
+                    scalar2=None,
+                    op0=ALU.mult,
                 )
+                grouped[i] = tile_i
+
+        def quantise_row(i):
+            kind, number, rows = row_tile(i)
+            if kind == "x":
+                quantise(x_codes, x_scales, number * 256, 256, grouped[i][:])
             else:
-                i = rows[0][1]
-                cd, sc = (xc, xs) if kind == "x" else (w4c, w4s)
-                nc.vector.quantize_mx(
-                    out=cd[:, i * 256 : (i + 1) * 256].bitcast(FP8X4),
-                    scales=sc[:, i * 256 : (i + 1) * 256],
-                    in_=grps[rows[0]][:],
-                )
-            for r in rows:
-                done.add(("q", r))
-                done.add(("rel", ("xsc" if kind == "x" else "grp", r)))
-            return True
+                quantise(w4_codes, w4_scales, number * 256, 256, grouped[i][:])
 
-        def op_mm1(unit, eng):
-            g, t = unit
-            need = [("q", ("x", t))] + [("q", ("w4", g * 4 + j)) for j in range(4)]
-            if not have(need) or not slot_free(mm_hist, N_MM):
-                return False
-            bank = ps_mm.tile([P, 512], F32, name="mm", tag="mm")
+        def layer1_matmul(g, t):
+            bank = mm_pool.tile([P, UNIT], F32, name="mm_bank", tag="mm_bank")
             for j in range(4):
-                for kg in range(2):
-                    wo = ((g * 4 + j) * 2 + kg) * P
-                    xo = (t * 2 + kg) * P
-                    nc.tensor.matmul_mx(
-                        out=bank[:, j * P : (j + 1) * P],
-                        lhsT=w4c[:, wo : wo + P].bitcast(FP8X4),
-                        lhsT_scale=w4s[:, wo : wo + P],
-                        rhs=xc[:, xo : xo + P].bitcast(FP8X4),
-                        rhs_scale=xs[:, xo : xo + P],
-                        start=(kg == 0),
-                        stop=(kg == 1),
+                for c in range(2):
+                    product(
+                        bank[:, j * P : (j + 1) * P],
+                        (w4_codes, w4_scales),
+                        ((4 * g + j) * 2 + c) * P,
+                        (x_codes, x_scales),
+                        (t * 2 + c) * P,
+                        P,
+                        c,
                     )
-            banks[("l1", unit)] = bank
-            mm_hist.append(("l1", unit))
-            done.add(("mm1", unit))
-            return True
+            mm_banks[(g, t)] = bank
 
-        def op_v1(unit, eng):
-            if ("mm1", unit) not in done:
-                return False
-            g, t = unit
+        def layer1_bias(g, t):
             nc.vector.tensor_tensor(
                 out=v_all[:, g, t, :].rearrange("p (w j) -> p w j", j=4),
-                in0=banks[("l1", unit)][:].rearrange("p (j w) -> p w j", j=4),
-                in1=b4g[:, g * 4 : (g + 1) * 4].unsqueeze(1).to_broadcast([P, P, 4]),
+                in0=mm_banks[(g, t)][:].rearrange("p (j w) -> p w j", j=4),
+                in1=b4_f32[:, 4 * g : 4 * g + 4].unsqueeze(1).to_broadcast([P, P, 4]),
                 op=ALU.add,
             )
-            done.add(("rel", ("l1", unit)))
-            done.add(("v1", unit))
-            return True
 
-        def sigmoid(units):
-            nc.scalar.activation(
-                out=view(s_all, units), in_=view(v_all, units), func=ACT.Sigmoid, scale=-100.0
+        entries = ((0, FIRST_X), (1, N_ROWS))
+        for step in range(N_ROWS + NT + LAG_SIGMOID):
+            for lag, stage in (
+                (LAG_SIGMOID, sigmoid),
+                (LAG_BIAS, layer1_bias),
+                (LAG_MATMUL, layer1_matmul),
+            ):
+                for g, entry in entries:
+                    if 0 <= step - entry - lag < NT:
+                        stage(g, step - entry - lag)
+            for lag, stage in (
+                (LAG_QUANTISE, quantise_row),
+                (LAG_SCALE, scale_row),
+                (LAG_COPY, copy_row),
+            ):
+                if 0 <= step - lag < N_ROWS:
+                    stage(step - lag)
+            if step == FIRST_X:
+                nc.vector.tensor_copy(
+                    out=x_raw[:, :, WHOLE_BLOCKS:H3_COLS], in_=h3_tail[:, :, 0 : H3_COLS - WHOLE_BLOCKS]
+                )
+                nc.vector.tensor_copy(out=x_raw[:, :, H3_COLS:K], in_=xin_sb[:, :, 0:3])
+                nc.vector.tensor_copy(out=b4_f32[:], in_=b4_bf[:])
+            if step < N_ROWS + 4:
+                tr_banks[step] = transpose_rows(row_tile(step)[2])
+
+        def copy_w5(engine_copy, i):
+            words = w5_grouped[i // 4][:].bitcast(F32).rearrange("p (g r u) -> p g r u", g=2, u=2)
+            engine_copy(
+                out=words[:, :, (i % 4) * P : (i % 4 + 1) * P, :], in_=bank_words(tr_banks[N_ROWS + i])
             )
 
-        def logarithm(units):
-            nc.scalar.activation(
-                out=view(s_all, units), in_=view(s_all, units), func=ACT.Ln, bias=delta[:, 0:1]
-            )
+        def quantise_w5(a):
+            quantise(w5_codes, w5_scales, a * 2 * UNIT, 2 * UNIT, w5_grouped[a][:])
 
-        def op_s1(units, eng):
-            if not have([("v1", u) for u in units]):
-                return False
-            sigmoid(units)
-            for u in units:
-                done.add(("s1", u))
-            return True
+        for i in range(4):
+            copy_w5(nc.vector.tensor_copy, i)
+        quantise_w5(0)
+        for i in range(4, NT):
+            tr_banks[N_ROWS + i] = transpose_rows(w5_raw[:, i, :])
 
-        def op_ln1(units, eng):
-            if not have([("s1", u) for u in units]):
-                return False
-            logarithm(units)
-            for u in units:
-                done.add(("ln1", u))
-            return True
+        units = [(a, t) for a in range(2) for t in range(NT)]
 
-        def op_f1(units, eng):
-            if not have([("ln1", u) for u in units]) or not slot_free(h4g_hist, N_H4G):
-                return False
-            h_t = h4g_pool.tile([P, K], BF16, name="h4g", tag="h4g", align_bytes=64)
-            nc.vector.scalar_tensor_tensor(
-                out=h_t[:, 0 : 512 * len(units)],
-                in0=view(s_all, units),
-                scalar=-0.01,
-                in1=view(v_all, units),
-                op0=ALU.mult,
-                op1=ALU.max,
-            )
-            grps[units] = h_t
-            h4g_hist.append(("h4g", units))
-            for u in units:
-                done.add(("f1", u))
-            return True
-
-        def op_q1(units, eng):
-            if not have([("f1", u) for u in units]):
-                return False
-            o = (units[0][0] * NT + units[0][1]) * P
-            n = len(units)
-            nc.vector.quantize_mx(
-                out=h4c[:, o : o + n * P].bitcast(FP8X4),
-                scales=h4s[:, o : o + n * P],
-                in_=grps[units][:, 0 : 512 * n],
-            )
-            done.add(("rel", ("h4g", units)))
-            for u in units:
-                done.add(("q1", u))
-            return True
-
-        def op_mm2(unit, eng):
-            t, hh = unit
-            need = [("q1", (0, t)), ("q1", (1, t))] + [("q", ("w5", hh * 4 + i)) for i in range(4)]
-            if not have(need) or not slot_free(mm_hist, N_MM):
-                return False
-            bank = ps_mm.tile([P, 512], F32, name="mm", tag="mm")
+        def layer2_matmul(a, t):
+            bank = mm_pool.tile([P, UNIT], F32, name="mm_bank", tag="mm_bank")
             for g in range(2):
-                ho = (g * NT + t) * P
-                wo = (hh * 2 + g) * 512
-                nc.tensor.matmul_mx(
-                    out=bank[:],
-                    lhsT=h4c[:, ho : ho + P].bitcast(FP8X4),
-                    lhsT_scale=h4s[:, ho : ho + P],
-                    rhs=w5c[:, wo : wo + 512].bitcast(FP8X4),
-                    rhs_scale=w5s[:, wo : wo + 512],
-                    start=(g == 0),
-                    stop=(g == 1),
+                product(
+                    bank[:],
+                    (h4_codes, h4_scales),
+                    (g * NT + t) * P,
+                    (w5_codes, w5_scales),
+                    (2 * a + g) * UNIT,
+                    UNIT,
+                    g,
                 )
-            banks[("l2", unit)] = bank
-            mm_hist.append(("l2", unit))
-            done.add(("mm2", unit))
-            return True
+            mm_banks[(a, t)] = bank
 
-        def op_v2(unit, eng):
-            if ("mm2", unit) not in done:
-                return False
-            t, hh = unit
+        def layer2_bias(a, t):
             nc.vector.tensor_tensor(
-                out=v_all[:, hh, t, :],
-                in0=banks[("l2", unit)][:],
-                in1=b5bc[:, hh * 512 : (hh + 1) * 512],
+                out=v_all[:, a, t, :],
+                in0=mm_banks[(a, t)][:],
+                in1=b5_all[:, a * UNIT : (a + 1) * UNIT],
                 op=ALU.add,
             )
-            done.add(("rel", ("l2", unit)))
-            done.add(("v2", unit))
-            return True
 
-        def op_s2(units, eng):
-            if not have([("v2", u) for u in units]):
-                return False
-            sigmoid(l2u(units))
-            for u in units:
-                done.add(("s2", u))
-            return True
+        for t in range(0, NT, 2):
+            h4_tiles = []
+            for g in range(2):
+                logs = s_all[:, g, t : t + 2, :].rearrange("p t c -> p (t c)")
+                logarithm(logs)
+                h4_bf = h4_pool.tile([P, 2 * UNIT], BF16, name="h4_bf", tag="h4_bf", align_bytes=64)
+                softplus_end(h4_bf[:], logs, v_all[:, g, t : t + 2, :].rearrange("p t c -> p (t c)"))
+                h4_tiles.append(h4_bf)
+            for g in range(2):
+                quantise(h4_codes, h4_scales, (g * NT + t) * P, 2 * P, h4_tiles[g][:])
+            if t < 4:
+                layer2_matmul(0, t)
+                layer2_matmul(0, t + 1)
+        for i in range(4, NT):
+            copy_w5(nc.scalar.copy, i)
+        for n, (a, t) in enumerate(units):
+            layer2_bias(a, t)
+            if n == 3:
+                quantise_w5(1)
+            if n + 4 < len(units):
+                layer2_matmul(units[n + 4][0], units[n + 4][1])
+        for a, t in units:
+            sigmoid(a, t)
 
-        def op_ln2(units, eng):
-            if not have([("s2", u) for u in units]):
-                return False
-            logarithm(l2u(units))
-            for u in units:
-                done.add(("ln2", u))
-            return True
-
-        def op_f2(units, eng):
-            if not have([("ln2", u) for u in units]):
-                return False
-            where = l2u(units)
-            nc.vector.scalar_tensor_tensor(
-                out=view(s_all, where),
-                in0=view(s_all, where),
-                scalar=-0.01,
-                in1=view(v_all, where),
-                op0=ALU.mult,
-                op1=ALU.max,
+        for a, t in units:
+            logarithm(s_all[:, a, t, :])
+            softplus_end(s_all[:, a, t, :], s_all[:, a, t, :], v_all[:, a, t, :])
+            nc.sync.dma_start(
+                out=out[t * P : (t + 1) * P, a * UNIT : (a + 1) * UNIT], in_=s_all[:, a, t, :]
             )
-            t = units[0][0]
-            if len(units) == 1:
-                hh = units[0][1]
-                nc.sync.dma_start(
-                    out=out[t * P : (t + 1) * P, hh * 512 : (hh + 1) * 512],
-                    in_=s_all[:, hh, t, :],
-                )
-            else:
-                nc.sync.dma_start(
-                    out=out[t * P : (t + 1) * P, :].rearrange("p (h c) -> p h c", h=2),
-                    in_=s_all[:, :, t, :],
-                )
-            return True
-
-        ops = {
-            "fix": op_fix, "t": op_t, "e": op_e, "m": op_m, "q": op_q, "mm1": op_mm1,
-            "v1": op_v1, "s1": op_s1, "ln1": op_ln1, "f1": op_f1, "q1": op_q1,
-            "mm2": op_mm2, "v2": op_v2, "s2": op_s2, "ln2": op_ln2, "f2": op_f2,
-        }
-        queues = (("pe", PE_ORDER), ("act", ACT_ORDER), ("dve", DVE_ORDER))
-        pos = [0, 0, 0]
-        total = len(PE_ORDER) + len(ACT_ORDER) + len(DVE_ORDER)
-        for sweep in range(total):
-            for qi, (eng, order) in enumerate(queues):
-                while pos[qi] < len(order) and ops[order[pos[qi]][0]](order[pos[qi]][1], eng):
-                    pos[qi] += 1
-        assert sum(pos) == total

@@ -29,7 +29,7 @@ LAG_MATMUL = 4
 LAG_BIAS = 6
 LAG_SIGMOID = 8
 N_ROWS = 16
-FIRST_X = 4
+UNIT_ENTRIES = ((0, 11), (1, 19))
 
 
 def tile_implicitnet_pa_kernel(tc, h3, x_in, W4, b4, W5, b5, out):
@@ -76,14 +76,12 @@ def tile_implicitnet_pa_kernel(tc, h3, x_in, W4, b4, W5, b5, out):
             pair = W4[(i // 2) * 256 : (i // 2 + 1) * 256, :].rearrange("(p e) k -> p e k", e=2)
             nc.sync.dma_start(out=w4_raw[:, i, :], in_=pair[:, i % 2, :])
 
-        for i in range(4):
-            load_w4(i)
-        nc.sync.dma_start(
+        nc.scalar.dma_start(
             out=h3_tail[:, :, 0 : H3_COLS - WHOLE_BLOCKS],
             in_=h3[:, WHOLE_BLOCKS:H3_COLS].rearrange("(t p) c -> p t c", p=P),
         )
-        nc.sync.dma_start(out=xin_sb[:, :, 0:3], in_=x_in.rearrange("(t p) c -> p t c", p=P))
-        nc.sync.dma_start(
+        nc.scalar.dma_start(out=xin_sb[:, :, 0:3], in_=x_in.rearrange("(t p) c -> p t c", p=P))
+        nc.scalar.dma_start(
             out=b4_bf[:].rearrange("p (a e) -> p a e", e=2),
             in_=b4.rearrange("(a p e) -> p a e", p=P, e=2),
         )
@@ -91,7 +89,7 @@ def tile_implicitnet_pa_kernel(tc, h3, x_in, W4, b4, W5, b5, out):
             nc.sync.dma_start(
                 out=x_raw[:, t, 0:WHOLE_BLOCKS], in_=h3[t * P : (t + 1) * P, 0:WHOLE_BLOCKS]
             )
-        for i in range(4, NT):
+        for i in range(NT):
             load_w4(i)
         for i in range(0, NT, 2):
             nc.sync.dma_start(
@@ -147,13 +145,9 @@ def tile_implicitnet_pa_kernel(tc, h3, x_in, W4, b4, W5, b5, out):
             )
 
         def row_tile(i):
-            if i < FIRST_X:
-                return "w4", i, w4_raw[:, i, :]
-            if i < FIRST_X + NT:
-                return "x", i - FIRST_X, x_raw[:, i - FIRST_X, :]
-            if i < N_ROWS:
-                return "w4", i - NT, w4_raw[:, i - NT, :]
-            return "w5", i - N_ROWS, w5_raw[:, i - N_ROWS, :]
+            if i < NT:
+                return "x", i, x_raw[:, i, :]
+            return "w4", i - NT, w4_raw[:, i - NT, :]
 
         tr_banks = {}
         mm_banks = {}
@@ -209,14 +203,18 @@ def tile_implicitnet_pa_kernel(tc, h3, x_in, W4, b4, W5, b5, out):
                 op=ALU.add,
             )
 
-        entries = ((0, FIRST_X), (1, N_ROWS))
-        for step in range(N_ROWS + NT + LAG_SIGMOID):
+        nc.vector.tensor_copy(
+            out=x_raw[:, :, WHOLE_BLOCKS:H3_COLS], in_=h3_tail[:, :, 0 : H3_COLS - WHOLE_BLOCKS]
+        )
+        nc.vector.tensor_copy(out=x_raw[:, :, H3_COLS:K], in_=xin_sb[:, :, 0:3])
+        nc.vector.tensor_copy(out=b4_f32[:], in_=b4_bf[:])
+        for step in range(UNIT_ENTRIES[1][1] + NT + LAG_SIGMOID):
             for lag, stage in (
                 (LAG_SIGMOID, sigmoid),
                 (LAG_BIAS, layer1_bias),
                 (LAG_MATMUL, layer1_matmul),
             ):
-                for g, entry in entries:
+                for g, entry in UNIT_ENTRIES:
                     if 0 <= step - entry - lag < NT:
                         stage(g, step - entry - lag)
             for lag, stage in (
@@ -226,13 +224,7 @@ def tile_implicitnet_pa_kernel(tc, h3, x_in, W4, b4, W5, b5, out):
             ):
                 if 0 <= step - lag < N_ROWS:
                     stage(step - lag)
-            if step == FIRST_X:
-                nc.vector.tensor_copy(
-                    out=x_raw[:, :, WHOLE_BLOCKS:H3_COLS], in_=h3_tail[:, :, 0 : H3_COLS - WHOLE_BLOCKS]
-                )
-                nc.vector.tensor_copy(out=x_raw[:, :, H3_COLS:K], in_=xin_sb[:, :, 0:3])
-                nc.vector.tensor_copy(out=b4_f32[:], in_=b4_bf[:])
-            if step < N_ROWS + 4:
+            if step < N_ROWS:
                 tr_banks[step] = transpose_rows(row_tile(step)[2])
 
         def copy_w5(engine_copy, i):
@@ -244,6 +236,8 @@ def tile_implicitnet_pa_kernel(tc, h3, x_in, W4, b4, W5, b5, out):
         def quantise_w5(a):
             quantise(w5_codes, w5_scales, a * 2 * UNIT, 2 * UNIT, w5_grouped[a][:])
 
+        for i in range(4):
+            tr_banks[N_ROWS + i] = transpose_rows(w5_raw[:, i, :])
         for i in range(4):
             copy_w5(nc.vector.tensor_copy, i)
         quantise_w5(0)

@@ -24,10 +24,10 @@ LN_FLOOR = 2.0 ** -60
 
 LAG_COPY = 1
 LAG_SCALE = 2
-LAG_QUANTISE = 3
-LAG_MATMUL = 4
-LAG_BIAS = 6
-LAG_SIGMOID = 8
+LAG_QUANTISE = 4
+LAG_MATMUL = 5
+LAG_BIAS = 7
+LAG_SIGMOID = 9
 N_ROWS = 16
 UNIT_ENTRIES = ((0, 11), (1, 19))
 
@@ -174,7 +174,7 @@ def tile_implicitnet_pa_kernel(tc, h3, x_in, W4, b4, W5, b5, out):
                 grouped[i] = tile_i
 
         def quantise_row(i):
-            kind, number, rows = row_tile(i)
+            kind, number = row_tile(i)[0:2]
             if kind == "x":
                 quantise(x_codes, x_scales, number * 256, 256, grouped[i][:])
             else:

@@ -28,6 +28,7 @@ LAG_QUANTISE = 4
 LAG_MATMUL = 5
 LAG_BIAS = 7
 LAG_SIGMOID = 9
+B4_STEP = 7
 N_ROWS = 16
 UNIT_ENTRIES = ((0, 11), (1, 19))
 
@@ -49,10 +50,10 @@ def tile_implicitnet_pa_kernel(tc, h3, x_in, W4, b4, W5, b5, out):
 
         x_raw = keep.tile([P, NT, K], BF16, name="x_raw")
         h3_tail = keep.tile([P, NT, 16], BF16, name="h3_tail")
-        xin_sb = keep.tile([P, NT, 4], BF16, name="xin_sb")
+        xin_sb = keep.tile([P, NT * 3], BF16, name="xin_sb")
         w4_raw = keep.tile([P, NT, K], BF16, name="w4_raw")
         w5_raw = keep.tile([P, NT, K], BF16, name="w5_raw")
-        b4_bf = keep.tile([P, NT], BF16, name="b4_bf")
+        b4_rows = keep.tile([P, 2 * P], BF16, name="b4_rows")
         b4_f32 = keep.tile([P, NT], F32, name="b4_f32")
         b5_all = keep.tile([P, K], BF16, name="b5_all")
         ln_floor = keep.tile([P, 1], F32, name="ln_floor")
@@ -78,16 +79,15 @@ def tile_implicitnet_pa_kernel(tc, h3, x_in, W4, b4, W5, b5, out):
 
         nc.scalar.dma_start(
             out=h3_tail[:, :, 0 : H3_COLS - WHOLE_BLOCKS],
-            in_=h3[:, WHOLE_BLOCKS:H3_COLS].rearrange("(t p) c -> p t c", p=P),
+            in_=h3[:, WHOLE_BLOCKS:H3_COLS].rearrange("(p t) c -> p t c", t=NT),
         )
-        nc.scalar.dma_start(out=xin_sb[:, :, 0:3], in_=x_in.rearrange("(t p) c -> p t c", p=P))
-        nc.scalar.dma_start(
-            out=b4_bf[:].rearrange("p (a e) -> p a e", e=2),
-            in_=b4.rearrange("(a p e) -> p a e", p=P, e=2),
-        )
+        nc.scalar.dma_start(out=xin_sb[:], in_=x_in.rearrange("(p t) c -> p (t c)", t=NT))
+        nc.vector.memset(b4_rows[:], 0.0)
+        nc.scalar.dma_start(out=b4_rows[0:4, :], in_=b4.rearrange("(a w) -> a w", a=4))
         for t in range(NT):
             nc.sync.dma_start(
-                out=x_raw[:, t, 0:WHOLE_BLOCKS], in_=h3[t * P : (t + 1) * P, 0:WHOLE_BLOCKS]
+                out=x_raw[:, t, 0:WHOLE_BLOCKS],
+                in_=h3[:, 0:WHOLE_BLOCKS].rearrange("(p t) c -> p t c", t=NT)[:, t, :],
             )
         for i in range(NT):
             load_w4(i)
@@ -206,8 +206,9 @@ def tile_implicitnet_pa_kernel(tc, h3, x_in, W4, b4, W5, b5, out):
         nc.vector.tensor_copy(
             out=x_raw[:, :, WHOLE_BLOCKS:H3_COLS], in_=h3_tail[:, :, 0 : H3_COLS - WHOLE_BLOCKS]
         )
-        nc.vector.tensor_copy(out=x_raw[:, :, H3_COLS:K], in_=xin_sb[:, :, 0:3])
-        nc.vector.tensor_copy(out=b4_f32[:], in_=b4_bf[:])
+        nc.vector.tensor_copy(
+            out=x_raw[:, :, H3_COLS:K], in_=xin_sb[:].rearrange("p (t c) -> p t c", c=3)
+        )
         for step in range(UNIT_ENTRIES[1][1] + NT + LAG_SIGMOID):
             for lag, stage in (
                 (LAG_SIGMOID, sigmoid),
@@ -226,6 +227,11 @@ def tile_implicitnet_pa_kernel(tc, h3, x_in, W4, b4, W5, b5, out):
                     stage(step - lag)
             if step < N_ROWS:
                 tr_banks[step] = transpose_rows(row_tile(step)[2])
+            if step == B4_STEP:
+                b4_bank = tr_pool.tile([P, UNIT], F32, name="tr_bank", tag="tr_bank")
+                nc.tensor.transpose(b4_bank[:, 0:P], b4_rows[:].bitcast(F32), ident[:])
+            if step == B4_STEP + 3:
+                nc.vector.tensor_copy(out=b4_f32[:], in_=b4_bank[:, 0:4].bitcast(BF16))
 
         def copy_w5(engine_copy, i):
             words = w5_grouped[i // 4][:].bitcast(F32).rearrange("p (g r u) -> p g r u", g=2, u=2)
@@ -296,5 +302,6 @@ def tile_implicitnet_pa_kernel(tc, h3, x_in, W4, b4, W5, b5, out):
             logarithm(s_all[:, a, t, :])
             softplus_end(s_all[:, a, t, :], s_all[:, a, t, :], v_all[:, a, t, :])
             nc.sync.dma_start(
-                out=out[t * P : (t + 1) * P, a * UNIT : (a + 1) * UNIT], in_=s_all[:, a, t, :]
+                out=out[:, a * UNIT : (a + 1) * UNIT].rearrange("(p t) c -> p t c", t=NT)[:, t, :],
+                in_=s_all[:, a, t, :],
             )

@@ -19,15 +19,15 @@ K = 1024
 NT = 8
 UNIT = 512
 H3_COLS = 1021
-WHOLE_BLOCKS = 1008
 LN_FLOOR = 2.0 ** -60
 
 LAG_COPY = 1
-LAG_SCALE = 2
 LAG_QUANTISE = 4
 LAG_MATMUL = 5
 LAG_BIAS = 7
 LAG_SIGMOID = 9
+H3_LOADS = ((0, 1), (1, 1), (2, 2), (4, 2), (6, 2))
+X_AHEAD = 2
 B4_STEP = 7
 N_ROWS = 16
 UNIT_ENTRIES = ((0, 11), (1, 19))
@@ -38,7 +38,6 @@ def tile_implicitnet_pa_kernel(tc, h3, x_in, W4, b4, W5, b5, out):
     with ExitStack() as ctx:
         keep = ctx.enter_context(tc.tile_pool(name="keep", bufs=1))
         grouped_pool = ctx.enter_context(tc.tile_pool(name="grouped", bufs=6))
-        scaled_pool = ctx.enter_context(tc.tile_pool(name="scaled", bufs=4))
         h4_pool = ctx.enter_context(tc.tile_pool(name="h4", bufs=4))
         tr_pool = ctx.enter_context(tc.psum_pool(name="tr", bufs=4))
         mm_pool = ctx.enter_context(tc.psum_pool(name="mm", bufs=4))
@@ -48,8 +47,8 @@ def tile_implicitnet_pa_kernel(tc, h3, x_in, W4, b4, W5, b5, out):
 
         ctx.enter_context(tc.manual_schedule())
 
+        h3_rows = keep.tile([P, NT * K], BF16, name="h3_rows")
         x_raw = keep.tile([P, NT, K], BF16, name="x_raw")
-        h3_tail = keep.tile([P, NT, 16], BF16, name="h3_tail")
         xin_sb = keep.tile([P, NT * 3], BF16, name="xin_sb")
         w4_raw = keep.tile([P, NT, K], BF16, name="w4_raw")
         w5_raw = keep.tile([P, NT, K], BF16, name="w5_raw")
@@ -77,17 +76,13 @@ def tile_implicitnet_pa_kernel(tc, h3, x_in, W4, b4, W5, b5, out):
             pair = W4[(i // 2) * 256 : (i // 2 + 1) * 256, :].rearrange("(p e) k -> p e k", e=2)
             nc.sync.dma_start(out=w4_raw[:, i, :], in_=pair[:, i % 2, :])
 
-        nc.scalar.dma_start(
-            out=h3_tail[:, :, 0 : H3_COLS - WHOLE_BLOCKS],
-            in_=h3[:, WHOLE_BLOCKS:H3_COLS].rearrange("(p t) c -> p t c", t=NT),
-        )
         nc.scalar.dma_start(out=xin_sb[:], in_=x_in.rearrange("(p t) c -> p (t c)", t=NT))
         nc.vector.memset(b4_rows[:], 0.0)
         nc.scalar.dma_start(out=b4_rows[0:4, :], in_=b4.rearrange("(a w) -> a w", a=4))
-        for t in range(NT):
+        for t, n in H3_LOADS:
             nc.sync.dma_start(
-                out=x_raw[:, t, 0:WHOLE_BLOCKS],
-                in_=h3[:, 0:WHOLE_BLOCKS].rearrange("(p t) c -> p t c", t=NT)[:, t, :],
+                out=h3_rows[:, t * K : t * K + n * H3_COLS],
+                in_=h3.rearrange("(p t) c -> p (t c)", t=NT)[:, t * H3_COLS : (t + n) * H3_COLS],
             )
         for i in range(NT):
             load_w4(i)
@@ -161,18 +156,6 @@ def tile_implicitnet_pa_kernel(tc, h3, x_in, W4, b4, W5, b5, out):
             )
             grouped[i] = tile_i
 
-        def scale_row(i):
-            if row_tile(i)[0] == "x":
-                tile_i = scaled_pool.tile([P, K], BF16, name="scaled", tag="scaled", align_bytes=64)
-                nc.vector.tensor_scalar(
-                    out=tile_i[:],
-                    in0=grouped[i][:],
-                    scalar1=math.sqrt(0.5),
-                    scalar2=None,
-                    op0=ALU.mult,
-                )
-                grouped[i] = tile_i
-
         def quantise_row(i):
             kind, number = row_tile(i)[0:2]
             if kind == "x":
@@ -203,12 +186,30 @@ def tile_implicitnet_pa_kernel(tc, h3, x_in, W4, b4, W5, b5, out):
                 op=ALU.add,
             )
 
-        nc.vector.tensor_copy(
-            out=x_raw[:, :, WHOLE_BLOCKS:H3_COLS], in_=h3_tail[:, :, 0 : H3_COLS - WHOLE_BLOCKS]
+        nc.vector.tensor_scalar(
+            out=x_raw[:, :, H3_COLS:K],
+            in0=xin_sb[:].rearrange("p (t c) -> p t c", c=3),
+            scalar1=math.sqrt(0.5),
+            scalar2=None,
+            op0=ALU.mult,
         )
-        nc.vector.tensor_copy(
-            out=x_raw[:, :, H3_COLS:K], in_=xin_sb[:].rearrange("p (t c) -> p t c", c=3)
-        )
+
+        h3_place = {}
+        for t, n in H3_LOADS:
+            for m in range(n):
+                h3_place[t + m] = t * K + m * H3_COLS
+
+        def scale_x(t):
+            nc.vector.tensor_scalar(
+                out=x_raw[:, t, 0:H3_COLS],
+                in0=h3_rows[:, h3_place[t] : h3_place[t] + H3_COLS],
+                scalar1=math.sqrt(0.5),
+                scalar2=None,
+                op0=ALU.mult,
+            )
+
+        for t in range(X_AHEAD):
+            scale_x(t)
         for step in range(UNIT_ENTRIES[1][1] + NT + LAG_SIGMOID):
             for lag, stage in (
                 (LAG_SIGMOID, sigmoid),
@@ -220,11 +221,12 @@ def tile_implicitnet_pa_kernel(tc, h3, x_in, W4, b4, W5, b5, out):
                         stage(g, step - entry - lag)
             for lag, stage in (
                 (LAG_QUANTISE, quantise_row),
-                (LAG_SCALE, scale_row),
                 (LAG_COPY, copy_row),
             ):
                 if 0 <= step - lag < N_ROWS:
                     stage(step - lag)
+            if step + X_AHEAD < NT:
+                scale_x(step + X_AHEAD)
             if step < N_ROWS:
                 tr_banks[step] = transpose_rows(row_tile(step)[2])
             if step == B4_STEP:

@@ -27,6 +27,7 @@ LAG_MATMUL = 5
 LAG_BIAS = 7
 LAG_SIGMOID = 9
 H3_LOADS = ((0, 1), (1, 1), (2, 2), (4, 2), (6, 2))
+STORE_PLACES = (1, 1, 2, 2, 2, 2, 2, 2, 1, 1)
 X_AHEAD = 2
 B4_STEP = 7
 N_ROWS = 16
@@ -130,6 +131,9 @@ def tile_implicitnet_pa_kernel(tc, h3, x_in, W4, b4, W5, b5, out):
             nc.scalar.activation(
                 out=s_all[:, a, t, :], in_=v_all[:, a, t, :], func=ACT.Sigmoid, scale=-100.0
             )
+
+        v_rows = v_all[:].rearrange("p g t c -> p (g t) c")
+        s_rows = s_all[:].rearrange("p g t c -> p (g t) c")
 
         def logarithm(cells):
             nc.scalar.activation(out=cells, in_=cells, func=ACT.Ln, bias=ln_floor[:, 0:1])
@@ -270,7 +274,7 @@ def tile_implicitnet_pa_kernel(tc, h3, x_in, W4, b4, W5, b5, out):
 
         def layer2_bias(a, t):
             nc.vector.tensor_tensor(
-                out=v_all[:, a, t, :],
+                out=v_rows[:, 2 * t + a, :],
                 in0=mm_banks[(a, t)][:],
                 in1=b5_all[:, a * UNIT : (a + 1) * UNIT],
                 op=ALU.add,
@@ -298,12 +302,17 @@ def tile_implicitnet_pa_kernel(tc, h3, x_in, W4, b4, W5, b5, out):
             if n + 4 < len(units):
                 layer2_matmul(units[n + 4][0], units[n + 4][1])
         for a, t in units:
-            sigmoid(a, t)
-
-        for a, t in units:
-            logarithm(s_all[:, a, t, :])
-            softplus_end(s_all[:, a, t, :], s_all[:, a, t, :], v_all[:, a, t, :])
-            nc.sync.dma_start(
-                out=out[:, a * UNIT : (a + 1) * UNIT].rearrange("(p t) c -> p t c", t=NT)[:, t, :],
-                in_=s_all[:, a, t, :],
+            nc.scalar.activation(
+                out=s_rows[:, 2 * t + a, :], in_=v_rows[:, 2 * t + a, :], func=ACT.Sigmoid, scale=-100.0
             )
+
+        first = 0
+        for width in STORE_PLACES:
+            for n in range(first, first + width):
+                logarithm(s_rows[:, n, :])
+                softplus_end(s_rows[:, n, :], s_rows[:, n, :], v_rows[:, n, :])
+            nc.sync.dma_start(
+                out=out.rearrange("(p t) c -> p (t c)", t=NT)[:, first * UNIT : (first + width) * UNIT],
+                in_=s_rows[:, first : first + width, :].rearrange("p n c -> p (n c)"),
+            )
+            first += width

@@ -27,7 +27,7 @@ LAG_MATMUL = 5
 LAG_BIAS = 7
 LAG_SIGMOID = 9
 H3_LOADS = ((0, 1), (1, 1), (2, 2), (4, 2), (6, 2))
-STORE_PLACES = (1, 1, 2, 2, 2, 2, 2, 2, 1, 1)
+STORE_PLACES = (2, 2, 2, 2, 2, 2, 2, 2)
 X_AHEAD = 2
 B4_STEP = 7
 N_ROWS = 16

import math
from contextlib import ExitStack

import concourse.mybir as mybir
from concourse.masks import make_identity

F32 = mybir.dt.float32
BF16 = mybir.dt.bfloat16
U32 = mybir.dt.uint32
U8 = mybir.dt.uint8
FP8X4 = mybir.dt.float8_e4m3fn_x4
ACT = mybir.ActivationFunctionType
ALU = mybir.AluOpType

FLOPS = 2 * 2 * 1024 * 1024 * 1024

P = 128
K = 1024
NT = 8
UNIT = 512
H3_COLS = 1021
LN_FLOOR = 2.0 ** -60

LAG_COPY = 1
LAG_QUANTISE = 4
LAG_MATMUL = 5
LAG_BIAS = 7
LAG_SIGMOID = 9
H3_LOADS = ((0, 1), (1, 1), (2, 2), (4, 2), (6, 2))
STORE_PLACES = (2, 2, 2, 2, 2, 2, 2, 2)
X_AHEAD = 2
B4_STEP = 7
N_ROWS = 16
UNIT_ENTRIES = ((0, 11), (1, 19))


def tile_implicitnet_pa_kernel(tc, h3, x_in, W4, b4, W5, b5, out):
    nc = tc.nc
    with ExitStack() as ctx:
        keep = ctx.enter_context(tc.tile_pool(name="keep", bufs=1))
        grouped_pool = ctx.enter_context(tc.tile_pool(name="grouped", bufs=6))
        h4_pool = ctx.enter_context(tc.tile_pool(name="h4", bufs=4))
        tr_pool = ctx.enter_context(tc.psum_pool(name="tr", bufs=4))
        mm_pool = ctx.enter_context(tc.psum_pool(name="mm", bufs=4))

        ident = keep.tile([P, P], F32, name="ident")
        make_identity(nc, ident[:])

        ctx.enter_context(tc.manual_schedule())

        h3_rows = keep.tile([P, NT * K], BF16, name="h3_rows")
        x_raw = keep.tile([P, NT, K], BF16, name="x_raw")
        xin_sb = keep.tile([P, NT * 3], BF16, name="xin_sb")
        w4_raw = keep.tile([P, NT, K], BF16, name="w4_raw")
        w5_raw = keep.tile([P, NT, K], BF16, name="w5_raw")
        b4_rows = keep.tile([P, 2 * P], BF16, name="b4_rows")
        b4_f32 = keep.tile([P, NT], F32, name="b4_f32")
        b5_all = keep.tile([P, K], BF16, name="b5_all")
        ln_floor = keep.tile([P, 1], F32, name="ln_floor")
        warm = keep.tile([P, 1], F32, name="warm")

        x_codes = keep.tile([P, NT * 256], U32, name="x_codes", align_bytes=64)
        x_scales = keep.tile([P, NT * 256], U8, name="x_scales", align_bytes=64)
        w4_codes = keep.tile([P, NT * 256], U32, name="w4_codes", align_bytes=64)
        w4_scales = keep.tile([P, NT * 256], U8, name="w4_scales", align_bytes=64)
        h4_codes = keep.tile([P, 2 * NT * P], U32, name="h4_codes", align_bytes=64)
        h4_scales = keep.tile([P, 2 * NT * P], U8, name="h4_scales", align_bytes=64)
        w5_codes = keep.tile([P, 4 * UNIT], U32, name="w5_codes", align_bytes=64)
        w5_scales = keep.tile([P, 4 * UNIT], U8, name="w5_scales", align_bytes=64)
        w5_grouped = [
            keep.tile([P, 4 * K], BF16, name="w5_grouped%d" % a, align_bytes=64) for a in range(2)
        ]
        v_all = keep.tile([P, 2, NT, UNIT], F32, name="v_all")
        s_all = keep.tile([P, 2, NT, UNIT], F32, name="s_all")

        def load_w4(i):
            pair = W4[(i // 2) * 256 : (i // 2 + 1) * 256, :].rearrange("(p e) k -> p e k", e=2)
            nc.sync.dma_start(out=w4_raw[:, i, :], in_=pair[:, i % 2, :])

        nc.scalar.dma_start(out=xin_sb[:], in_=x_in.rearrange("(p t) c -> p (t c)", t=NT))
        nc.vector.memset(b4_rows[:], 0.0)
        nc.scalar.dma_start(out=b4_rows[0:4, :], in_=b4.rearrange("(a w) -> a w", a=4))
        for t, n in H3_LOADS:
            nc.sync.dma_start(
                out=h3_rows[:, t * K : t * K + n * H3_COLS],
                in_=h3.rearrange("(p t) c -> p (t c)", t=NT)[:, t * H3_COLS : (t + n) * H3_COLS],
            )
        for i in range(NT):
            load_w4(i)
        for i in range(0, NT, 2):
            nc.sync.dma_start(
                out=w5_raw[:, i : i + 2, :],
                in_=W5[i * P : (i + 2) * P, :].rearrange("(t p) k -> p t k", p=P),
            )
        nc.sync.dma_start(out=b5_all[:], in_=b5.partition_broadcast(P))

        nc.vector.memset(warm[:], 0.0)
        nc.vector.memset(ln_floor[:], LN_FLOOR)
        nc.scalar.activation(out=warm[:], in_=warm[:], func=ACT.Sigmoid)

        def transpose_rows(rows):
            words = rows.bitcast(F32)
            bank = tr_pool.tile([P, UNIT], F32, name="tr_bank", tag="tr_bank")
            for cu in range(4):
                cols = slice(cu * P, (cu + 1) * P)
                nc.tensor.transpose(bank[:, cols], words[:, cols], ident[:])
            return bank

        def bank_words(bank):
            return bank[:].rearrange("p (c u r) -> p c r u", c=2, u=2)

        def quantise(codes, scales, first, width, values):
            nc.vector.quantize_mx(
                out=codes[:, first : first + width].bitcast(FP8X4),
                scales=scales[:, first : first + width],
                in_=values,
            )

        def product(bank_cols, lhs, lhs_first, rhs, rhs_first, width, c):
            nc.tensor.matmul_mx(
                out=bank_cols,
                lhsT=lhs[0][:, lhs_first : lhs_first + P].bitcast(FP8X4),
                lhsT_scale=lhs[1][:, lhs_first : lhs_first + P],
                rhs=rhs[0][:, rhs_first : rhs_first + width].bitcast(FP8X4),
                rhs_scale=rhs[1][:, rhs_first : rhs_first + width],
                start=(c == 0),
                stop=(c == 1),
            )

        def sigmoid(a, t):
            nc.scalar.activation(
                out=s_all[:, a, t, :], in_=v_all[:, a, t, :], func=ACT.Sigmoid, scale=-100.0
            )

        v_rows = v_all[:].rearrange("p g t c -> p (g t) c")
        s_rows = s_all[:].rearrange("p g t c -> p (g t) c")

        def logarithm(cells):
            nc.scalar.activation(out=cells, in_=cells, func=ACT.Ln, bias=ln_floor[:, 0:1])

        def softplus_end(dst, logs, pre):
            nc.vector.scalar_tensor_tensor(
                out=dst, in0=logs, scalar=-0.01, in1=pre, op0=ALU.mult, op1=ALU.max
            )

        def row_tile(i):
            if i < NT:
                return "x", i, x_raw[:, i, :]
            return "w4", i - NT, w4_raw[:, i - NT, :]

        tr_banks = {}
        mm_banks = {}
        grouped = {}

        def copy_row(i):
            tile_i = grouped_pool.tile([P, K], BF16, name="grouped", tag="grouped", align_bytes=64)
            nc.scalar.copy(
                out=tile_i[:].bitcast(F32).rearrange("p (c r u) -> p c r u", c=2, u=2),
                in_=bank_words(tr_banks[i]),
            )
            grouped[i] = tile_i

        def quantise_row(i):
            kind, number = row_tile(i)[0:2]
            if kind == "x":
                quantise(x_codes, x_scales, number * 256, 256, grouped[i][:])
            else:
                quantise(w4_codes, w4_scales, number * 256, 256, grouped[i][:])

        def layer1_matmul(g, t):
            bank = mm_pool.tile([P, UNIT], F32, name="mm_bank", tag="mm_bank")
            for j in range(4):
                for c in range(2):
                    product(
                        bank[:, j * P : (j + 1) * P],
                        (w4_codes, w4_scales),
                        ((4 * g + j) * 2 + c) * P,
                        (x_codes, x_scales),
                        (t * 2 + c) * P,
                        P,
                        c,
                    )
            mm_banks[(g, t)] = bank

        def layer1_bias(g, t):
            nc.vector.tensor_tensor(
                out=v_all[:, g, t, :].rearrange("p (w j) -> p w j", j=4),
                in0=mm_banks[(g, t)][:].rearrange("p (j w) -> p w j", j=4),
                in1=b4_f32[:, 4 * g : 4 * g + 4].unsqueeze(1).to_broadcast([P, P, 4]),
                op=ALU.add,
            )

        nc.vector.tensor_scalar(
            out=x_raw[:, :, H3_COLS:K],
            in0=xin_sb[:].rearrange("p (t c) -> p t c", c=3),
            scalar1=math.sqrt(0.5),
            scalar2=None,
            op0=ALU.mult,
        )

        h3_place = {}
        for t, n in H3_LOADS:
            for m in range(n):
                h3_place[t + m] = t * K + m * H3_COLS

        def scale_x(t):
            nc.vector.tensor_scalar(
                out=x_raw[:, t, 0:H3_COLS],
                in0=h3_rows[:, h3_place[t] : h3_place[t] + H3_COLS],
                scalar1=math.sqrt(0.5),
                scalar2=None,
                op0=ALU.mult,
            )

        for t in range(X_AHEAD):
            scale_x(t)
        for step in range(UNIT_ENTRIES[1][1] + NT + LAG_SIGMOID):
            for lag, stage in (
                (LAG_SIGMOID, sigmoid),
                (LAG_BIAS, layer1_bias),
                (LAG_MATMUL, layer1_matmul),
            ):
                for g, entry in UNIT_ENTRIES:
                    if 0 <= step - entry - lag < NT:
                        stage(g, step - entry - lag)
            for lag, stage in (
                (LAG_QUANTISE, quantise_row),
                (LAG_COPY, copy_row),
            ):
                if 0 <= step - lag < N_ROWS:
                    stage(step - lag)
            if step + X_AHEAD < NT:
                scale_x(step + X_AHEAD)
            if step < N_ROWS:
                tr_banks[step] = transpose_rows(row_tile(step)[2])
            if step == B4_STEP:
                b4_bank = tr_pool.tile([P, UNIT], F32, name="tr_bank", tag="tr_bank")
                nc.tensor.transpose(b4_bank[:, 0:P], b4_rows[:].bitcast(F32), ident[:])
            if step == B4_STEP + 3:
                nc.vector.tensor_copy(out=b4_f32[:], in_=b4_bank[:, 0:4].bitcast(BF16))

        def copy_w5(engine_copy, i):
            words = w5_grouped[i // 4][:].bitcast(F32).rearrange("p (g r u) -> p g r u", g=2, u=2)
            engine_copy(
                out=words[:, :, (i % 4) * P : (i % 4 + 1) * P, :], in_=bank_words(tr_banks[N_ROWS + i])
            )

        def quantise_w5(a):
            quantise(w5_codes, w5_scales, a * 2 * UNIT, 2 * UNIT, w5_grouped[a][:])

        for i in range(4):
            tr_banks[N_ROWS + i] = transpose_rows(w5_raw[:, i, :])
        for i in range(4):
            copy_w5(nc.vector.tensor_copy, i)
        quantise_w5(0)
        for i in range(4, NT):
            tr_banks[N_ROWS + i] = transpose_rows(w5_raw[:, i, :])

        units = [(a, t) for a in range(2) for t in range(NT)]

        def layer2_matmul(a, t):
            bank = mm_pool.tile([P, UNIT], F32, name="mm_bank", tag="mm_bank")
            for g in range(2):
                product(
                    bank[:],
                    (h4_codes, h4_scales),
                    (g * NT + t) * P,
                    (w5_codes, w5_scales),
                    (2 * a + g) * UNIT,
                    UNIT,
                    g,
                )
            mm_banks[(a, t)] = bank

        def layer2_bias(a, t):
            nc.vector.tensor_tensor(
                out=v_rows[:, 2 * t + a, :],
                in0=mm_banks[(a, t)][:],
                in1=b5_all[:, a * UNIT : (a + 1) * UNIT],
                op=ALU.add,
            )

        for t in range(0, NT, 2):
            h4_tiles = []
            for g in range(2):
                logs = s_all[:, g, t : t + 2, :].rearrange("p t c -> p (t c)")
                logarithm(logs)
                h4_bf = h4_pool.tile([P, 2 * UNIT], BF16, name="h4_bf", tag="h4_bf", align_bytes=64)
                softplus_end(h4_bf[:], logs, v_all[:, g, t : t + 2, :].rearrange("p t c -> p (t c)"))
                h4_tiles.append(h4_bf)
            for g in range(2):
                quantise(h4_codes, h4_scales, (g * NT + t) * P, 2 * P, h4_tiles[g][:])
            if t < 4:
                layer2_matmul(0, t)
                layer2_matmul(0, t + 1)
        for i in range(4, NT):
            copy_w5(nc.scalar.copy, i)
        for n, (a, t) in enumerate(units):
            layer2_bias(a, t)
            if n == 3:
                quantise_w5(1)
            if n + 4 < len(units):
                layer2_matmul(units[n + 4][0], units[n + 4][1])
        for a, t in units:
            nc.scalar.activation(
                out=s_rows[:, 2 * t + a, :], in_=v_rows[:, 2 * t + a, :], func=ACT.Sigmoid, scale=-100.0
            )

        first = 0
        for width in STORE_PLACES:
            for n in range(first, first + width):
                logarithm(s_rows[:, n, :])
                softplus_end(s_rows[:, n, :], s_rows[:, n, :], v_rows[:, n, :])
            nc.sync.dma_start(
                out=out.rearrange("(p t) c -> p (t c)", t=NT)[:, first * UNIT : (first + width) * UNIT],
                in_=s_rows[:, first : first + width, :].rearrange("p n c -> p (n c)"),
            )
            first += width
